import numpy as np
import ml_dtypes


def mxq(x, axis, fmt="e4m3"):
    dtype, down = {"e4m3": (ml_dtypes.float8_e4m3fn, 7), "e5m2": (ml_dtypes.float8_e5m2, 14)}[fmt]
    v = np.moveaxis(np.asarray(x, np.float32).astype(ml_dtypes.bfloat16).astype(np.float64), axis, -1)
    blocks = v.reshape(v.shape[:-1] + (-1, 32))
    amax = np.abs(blocks).max(-1, keepdims=True)
    byte = np.maximum(np.where(amax > 0, np.frexp(amax)[1] - 1 + 127, 0) - down, 1)
    scale = np.exp2(byte - 127.0)
    codes = (blocks / scale).astype(np.float32).astype(dtype).astype(np.float64)
    return np.moveaxis((codes * scale).reshape(v.shape), -1, axis)


WIDE = False


def mx_kscale(k):
    if not WIDE:
        return np.ones(k)
    levels = np.array([10, -10, 5, -5, 0])
    a = np.random.permutation(np.resize(levels, k // 512 * 4)).reshape(k // 512, 4)
    idx = np.arange(k)
    return np.exp2(a[idx // 512, idx % 128 // 32])


BF16 = ml_dtypes.bfloat16


def bf(x):
    return np.asarray(x, np.float32).astype(BF16)


def f64(x):
    return np.asarray(x).astype(np.float64)


B, CIN, R, COUT, H, W, D, KS = 1, 512, 512, 512, 8, 16, 16, 3
P = H * W * D
PAD = (KS - 1) // 2


def slice_in_dim(t, a, b, axis):
    idx = [slice(None)] * t.ndim
    idx[axis] = slice(a, b)
    return t[tuple(idx)]


def axis_contract(t, U, axis):
    L = t.shape[axis] - (KS - 1)
    rshape = (1, U.shape[1], 1, 1, 1)
    acc = slice_in_dim(t, 0, L, axis) * U[0].reshape(rshape)
    for k in range(1, KS):
        acc = acc + slice_in_dim(t, k, k + L, axis) * U[k].reshape(rshape)
    return acc


def setup_inputs():
    s, t = mx_kscale(CIN), mx_kscale(R)
    return {"x": bf(np.random.standard_normal((B, CIN, H, W, D)) * s[None, :, None, None, None]),
            "U_kh": bf(np.random.standard_normal((KS, R)) / np.sqrt(KS)),
            "U_kw": bf(np.random.standard_normal((KS, R)) / np.sqrt(KS)),
            "U_kd": bf(np.random.standard_normal((KS, R)) / np.sqrt(KS)),
            "U_c_in": bf(np.random.standard_normal((CIN, R)) / np.sqrt(CIN) / s[:, None] * t[None, :]),
            "U_c_out": bf(np.random.standard_normal((R, COUT)) / np.sqrt(R) / t[:, None]),
            "bias": bf(np.random.standard_normal(COUT) * 0.5)}


def reference(x, U_kh, U_kw, U_kd, U_c_in, U_c_out, bias):
    xq = mxq(f64(x), 1, "e4m3").reshape(B, CIN, P)
    y = (mxq(f64(U_c_in), 0, "e4m3").T @ xq).reshape(B, R, H, W, D)
    y = np.pad(y, ((0, 0), (0, 0), (PAD, PAD), (PAD, PAD), (PAD, PAD)))
    y = axis_contract(y, f64(U_kh), 2)
    y = axis_contract(y, f64(U_kw), 3)
    y = axis_contract(y, f64(U_kd), 4)
    out = (mxq(f64(U_c_out), 0, "e4m3").T @ mxq(y, 1, "e4m3").reshape(B, R, P)).reshape(B, COUT, H, W, D)
    return out + f64(bias)[None, :, None, None, None]

@@ -1,0 +1,408 @@
+from contextlib import ExitStack
+
+import concourse.mybir as mybir
+from concourse.masks import make_identity
+
+F32 = mybir.dt.float32
+BF16 = mybir.dt.bfloat16
+U32 = mybir.dt.uint32
+U8 = mybir.dt.uint8
+FP8X4 = mybir.dt.float8_e4m3fn_x4
+MULT = mybir.AluOpType.mult
+ADD = mybir.AluOpType.add
+COPY = mybir.ActivationFunctionType.Copy
+IDENT = mybir.ActivationFunctionType.Identity
+
+P = 128
+PACK = 4
+NPOS = 2048
+SLICE = 256
+ROW = 16
+CHUNK = 512
+NT = 4
+KH = 0
+KW = 3
+KD = 6
+KB = 9
+NSMALL = 10
+
+FLOPS = 2 * 2 * 512 * 512 * NPOS + 2 * 9 * 512 * NPOS
+
+XP = ((0, 256), (256, 256), (512, 512), (1024, 512), (1536, 512))
+HG = ((0, 256), (256, 512), (768, 512), (1792, 256), (1280, 256), (1536, 256))
+
+
+def tile_lowrankconv3d_kernel(tc, x, U_kh, U_kw, U_kd, U_c_in, U_c_out, bias, out):
+    nc = tc.nc
+    xv = x.rearrange("b c h w d -> (b c) (h w d)").rearrange("(p j) n -> p j n", j=PACK)
+    uinv = U_c_in.rearrange("(p j) r -> p j r", j=PACK)
+    uoutv = U_c_out.rearrange("(j p) o -> p j o", p=P)
+    outv = out.rearrange("b o h w d -> (b o) (h w d)")
+
+    with ExitStack() as ctx:
+        keep = ctx.enter_context(tc.tile_pool(name="keep", bufs=1))
+        xgp = ctx.enter_context(tc.tile_pool(name="xgp", bufs=1))
+        upool = ctx.enter_context(tc.tile_pool(name="upool", bufs=8))
+        zpool = ctx.enter_context(tc.tile_pool(name="zpool", bufs=8))
+        ypool = ctx.enter_context(tc.tile_pool(name="ypool", bufs=3))
+        opool = ctx.enter_context(tc.tile_pool(name="opool", bufs=6))
+        ps = ctx.enter_context(tc.psum_pool(name="ps", bufs=8))
+        ctx.enter_context(tc.manual_schedule())
+
+        small = keep.tile([P, 512], BF16, name="small")
+        warm = keep.tile([P, 8], F32, name="warm")
+        warm2 = keep.tile([P, 8], F32, name="warm2")
+        ident = keep.tile([P, P], BF16, name="ident")
+        taps = keep.tile([P, NT, NSMALL], F32, name="taps")
+        uin_raw = keep.tile([P, PACK, 512], BF16, name="uin_raw")
+        uin_g = keep.tile([P, 512, PACK], BF16, name="uin_g", align_bytes=64)
+        uin_c = keep.tile([P, 512], U32, name="uin_c", align_bytes=64)
+        uin_s = keep.tile([P, 512], U8, name="uin_s", align_bytes=64)
+        uout_raw = keep.tile([P, PACK, 512], BF16, name="uout_raw")
+        uout_g = keep.tile([P, 512, PACK], BF16, name="uout_g", align_bytes=64)
+        uout_c = keep.tile([P, 512], U32, name="uout_c", align_bytes=64)
+        uout_s = keep.tile([P, 512], U8, name="uout_s", align_bytes=64)
+        xraw = [keep.tile([P, PACK, XP[i][1]], BF16, name="xraw%d" % i) for i in range(len(XP))]
+        xc = [keep.tile([P, XP[i][1]], U32, name="xc%d" % i, align_bytes=64) for i in range(len(XP))]
+        xs = [keep.tile([P, XP[i][1]], U8, name="xs%d" % i, align_bytes=64) for i in range(len(XP))]
+        v = [keep.tile([P, NPOS], F32, name="v%d" % t) for t in range(NT)]
+        xg = {}
+        y0 = {}
+        u = {}
+        z = {}
+        y3 = {}
+        y3g = {}
+        yc = {}
+        ys = {}
+        po = {}
+
+        def tap(t, k):
+            return taps[:, t, k : k + 1]
+
+        def regroup(eng, dst, src):
+            if eng == "G":
+                nc.gpsimd.tensor_scalar(
+                    out=dst, in0=src.rearrange("p t w -> p w t"), scalar1=1.0, scalar2=0.0, op0=MULT, op1=ADD
+                )
+                return
+            d4 = dst.rearrange("p (c i) t -> p c t i", i=4)
+            s4 = src.rearrange("p t (c i) -> p c t i", i=4)
+            if eng == "V":
+                nc.vector.tensor_copy(out=d4, in_=s4)
+            else:
+                nc.scalar.copy(out=d4, in_=s4)
+
+        def quantise(codes, scales, grouped):
+            nc.vector.quantize_mx(
+                out=codes.bitcast(FP8X4), scales=scales, in_=grouped.rearrange("p w t -> p (w t)")
+            )
+
+        def x_regroup(i, eng, a=0, b=None):
+            w = XP[i][1]
+            if b is None:
+                b = w
+            if i not in xg:
+                xg[i] = xgp.tile([P, w, PACK], BF16, name="xg%d" % i, tag="xg", align_bytes=64)
+            regroup(eng, xg[i][:, a:b, :], xraw[i][:, :, a:b])
+
+        def x_quant(i):
+            quantise(xc[i][:], xs[i][:], xg[i][:])
+
+        def mm1(t, i):
+            w = XP[i][1]
+            y0[(t, i)] = ps.tile([P, w], F32, name="y0_%d_%d" % (t, i), tag="ps")
+            nc.tensor.matmul_mx(
+                out=y0[(t, i)][:],
+                lhsT=uin_c[:, t * P : (t + 1) * P].bitcast(FP8X4),
+                lhsT_scale=uin_s[:, t * P : (t + 1) * P],
+                rhs=xc[i][:].bitcast(FP8X4),
+                rhs_scale=xs[i][:],
+                start=True,
+                stop=True,
+            )
+
+        def d_centre(t, i):
+            lo, w = XP[i]
+            c = lo // CHUNK
+            o = lo % CHUNK
+            if (t, c) not in u:
+                u[(t, c)] = upool.tile([P, CHUNK], F32, name="u_%d_%d" % (t, c), tag="u")
+            nc.scalar.activation(out=u[(t, c)][:, o : o + w], in_=y0[(t, i)][:], func=COPY, scale=tap(t, KD + 1))
+
+        def d_side(t, i, k):
+            lo, w = XP[i]
+            c = lo // CHUNK
+            o = lo % CHUNK
+            uu = u[(t, c)][:, o : o + w].rearrange("p (r d) -> p r d", d=ROW)
+            yy = y0[(t, i)][:].rearrange("p (r d) -> p r d", d=ROW)
+            if k == 0:
+                dst, src = uu[:, :, 1:ROW], yy[:, :, 0 : ROW - 1]
+            else:
+                dst, src = uu[:, :, 0 : ROW - 1], yy[:, :, 1:ROW]
+            nc.vector.scalar_tensor_tensor(out=dst, in0=src, scalar=tap(t, KD + k), in1=dst, op0=MULT, op1=ADD)
+
+        def d_pair(a, b, i):
+            d_side(a, i, 0)
+            d_side(b, i, 0)
+            d_side(a, i, 2)
+            d_side(b, i, 2)
+
+        def w_centre(t, c):
+            nc.scalar.activation(
+                out=v[t][:, c * CHUNK : (c + 1) * CHUNK], in_=u[(t, c)][:], func=COPY, scale=tap(t, KW + 1)
+            )
+
+        def w_side(t, c, k):
+            vv = v[t][:, c * CHUNK : (c + 1) * CHUNK].rearrange("p (s n) -> p s n", n=SLICE)
+            uu = u[(t, c)][:].rearrange("p (s n) -> p s n", n=SLICE)
+            if k == 0:
+                dst, src = vv[:, :, ROW:SLICE], uu[:, :, 0 : SLICE - ROW]
+            else:
+                dst, src = vv[:, :, 0 : SLICE - ROW], uu[:, :, ROW:SLICE]
+            nc.vector.scalar_tensor_tensor(out=dst, in0=src, scalar=tap(t, KW + k), in1=dst, op0=MULT, op1=ADD)
+
+        def w_pair(a, b, c):
+            w_side(a, c, 0)
+            w_side(b, c, 0)
+            w_side(a, c, 2)
+            w_side(b, c, 2)
+
+        def h_centre(t, g):
+            lo, w = HG[g]
+            z[(t, g)] = zpool.tile([P, w], F32, name="z_%d_%d" % (t, g), tag="z")
+            nc.scalar.activation(out=z[(t, g)][:], in_=v[t][:, lo : lo + w], func=COPY, scale=tap(t, KH + 1))
+
+        def h_side(t, g, k):
+            lo, w = HG[g]
+            if g not in y3:
+                y3[g] = ypool.tile([P, NT, w], BF16, name="y3_%d" % g, tag="y3")
+            zz = z[(t, g)]
+            last = lo + w == NPOS
+            if k == 0:
+                a = max(lo, SLICE)
+                dst = y3[g][:, t, :] if last else zz[:, a - lo : w]
+                nc.vector.scalar_tensor_tensor(
+                    out=dst, in0=v[t][:, a - SLICE : lo + w - SLICE], scalar=tap(t, KH), in1=zz[:, a - lo : w],
+                    op0=MULT, op1=ADD,
+                )
+            else:
+                nc.vector.scalar_tensor_tensor(
+                    out=y3[g][:, t, :], in0=v[t][:, lo + SLICE : lo + w + SLICE], scalar=tap(t, KH + 2), in1=zz[:],
+                    op0=MULT, op1=ADD,
+                )
+
+        def h_pair(a, b, g):
+            h_side(a, g, 0)
+            h_side(b, g, 0)
+            h_side(a, g, 2)
+            h_side(b, g, 2)
+
+        def y_regroup(g, eng):
+            w = HG[g][1]
+            y3g[g] = ypool.tile([P, w, PACK], BF16, name="y3g_%d" % g, tag="y3g", align_bytes=64)
+            regroup(eng, y3g[g][:], y3[g][:])
+
+        def y_quant(g):
+            w = HG[g][1]
+            yc[g] = ypool.tile([P, w], U32, name="yc_%d" % g, tag="yc", align_bytes=64)
+            ys[g] = ypool.tile([P, w], U8, name="ys_%d" % g, tag="ys", align_bytes=64)
+            quantise(yc[g][:], ys[g][:], y3g[g][:])
+
+        def mm2(o, g):
+            w = HG[g][1]
+            po[(o, g)] = ps.tile([P, w], F32, name="po_%d_%d" % (o, g), tag="ps")
+            nc.tensor.matmul_mx(
+                out=po[(o, g)][:],
+                lhsT=uout_c[:, o * P : (o + 1) * P].bitcast(FP8X4),
+                lhsT_scale=uout_s[:, o * P : (o + 1) * P],
+                rhs=yc[g][:].bitcast(FP8X4),
+                rhs_scale=ys[g][:],
+                start=True,
+                stop=True,
+            )
+
+        def outp(o, g, eng):
+            lo, w = HG[g]
+            ost = opool.tile([P, w], F32, name="ost_%d_%d" % (o, g), tag="ost")
+            if eng == "V":
+                nc.vector.tensor_scalar(out=ost[:], in0=po[(o, g)][:], scalar1=tap(o, KB), scalar2=None, op0=ADD)
+            else:
+                nc.scalar.activation(out=ost[:], in_=po[(o, g)][:], func=IDENT, bias=tap(o, KB), scale=1.0)
+            nc.sync.dma_start(out=outv[o * P : (o + 1) * P, lo : lo + w], in_=ost[:])
+
+        nc.vector.memset(small[:], 0.0)
+        nc.vector.memset(warm[:], 0.0)
+        nc.scalar.dma_start(out=small[KD : KD + 3, :], in_=U_kd)
+        nc.scalar.dma_start(out=small[KW : KW + 3, :], in_=U_kw)
+        nc.scalar.dma_start(out=small[KH : KH + 3, :], in_=U_kh)
+        nc.scalar.dma_start(out=small[KB : KB + 1, :], in_=bias.rearrange("(a n) -> a n", a=1))
+        nc.scalar.activation(out=warm2[:], in_=warm[:], func=COPY, scale=1.0)
+        make_identity(nc, ident[:])
+        nc.sync.dma_start(out=xraw[0][:], in_=xv[:, :, XP[0][0] : XP[0][0] + XP[0][1]])
+        nc.sync.dma_start(out=uin_raw[:], in_=uinv)
+        for i in range(1, len(XP)):
+            nc.sync.dma_start(out=xraw[i][:], in_=xv[:, :, XP[i][0] : XP[i][0] + XP[i][1]])
+        nc.sync.dma_start(out=uout_raw[:], in_=uoutv)
+
+        x_regroup(0, "V")
+        x_quant(0)
+        regroup("V", uin_g[:, 0:256, :], uin_raw[:, :, 0:256])
+        regroup("S", uin_g[:, 256:512, :], uin_raw[:, :, 256:512])
+        tp = ps.tile([P, NT, P], BF16, name="tp", tag="ps")
+        for t in range(NT):
+            nc.tensor.transpose(tp[:, t, :], small[:, t * P : (t + 1) * P], ident[:])
+        nc.vector.tensor_copy(out=taps[:], in_=tp[:, :, 0:NSMALL])
+        quantise(uin_c[:, 0:256], uin_s[:, 0:256], uin_g[:, 0:256, :])
+        quantise(uin_c[:, 256:512], uin_s[:, 256:512], uin_g[:, 256:512, :])
+        x_regroup(1, "V")
+        x_quant(1)
+        for i in (0, 1):
+            for t in range(NT):
+                mm1(t, i)
+            for t in range(NT):
+                d_centre(t, i)
+        x_regroup(2, "G")
+
+        d_pair(0, 1, 0)
+        d_pair(2, 3, 0)
+        d_pair(0, 1, 1)
+        w_centre(0, 0)
+        w_centre(1, 0)
+        d_pair(2, 3, 1)
+        w_centre(2, 0)
+        w_centre(3, 0)
+        x_quant(2)
+        for t in range(NT):
+            mm1(t, 2)
+        w_pair(0, 1, 0)
+        h_centre(0, 0)
+        h_centre(1, 0)
+        d_centre(0, 2)
+        d_centre(1, 2)
+        w_pair(2, 3, 0)
+        h_centre(2, 0)
+        h_centre(3, 0)
+        d_centre(2, 2)
+        d_centre(3, 2)
+        for t in range(NT):
+            h_side(t, 0, 2)
+        x_regroup(3, "S", 0, 256)
+        x_regroup(3, "S", 256, 512)
+        y_regroup(0, "G")
+
+        d_pair(0, 1, 2)
+        w_centre(0, 1)
+        w_centre(1, 1)
+        regroup("S", uout_g[:, 0:256, :], uout_raw[:, :, 0:256])
+        x_quant(3)
+        d_pair(2, 3, 2)
+        w_centre(2, 1)
+        w_centre(3, 1)
+        regroup("S", uout_g[:, 256:512, :], uout_raw[:, :, 256:512])
+        y_quant(0)
+        for t in range(NT):
+            mm1(t, 3)
+        w_pair(0, 1, 1)
+        h_centre(0, 1)
+        h_centre(1, 1)
+        w_pair(2, 3, 1)
+        h_centre(2, 1)
+        h_centre(3, 1)
+        quantise(uout_c[:], uout_s[:], uout_g[:])
+        for o in range(NT):
+            mm2(o, 0)
+        h_pair(0, 1, 1)
+        d_centre(0, 3)
+        d_centre(1, 3)
+        outp(0, 0, "S")
+        outp(1, 0, "S")
+        h_pair(2, 3, 1)
+        d_centre(2, 3)
+        d_centre(3, 3)
+        outp(2, 0, "S")
+        outp(3, 0, "S")
+        y_regroup(1, "G")
+
+        d_pair(0, 1, 3)
+        w_centre(0, 2)
+        w_centre(1, 2)
+        x_regroup(4, "S", 0, 256)
+        d_pair(2, 3, 3)
+        w_centre(2, 2)
+        w_centre(3, 2)
+        x_regroup(4, "S", 256, 512)
+        y_quant(1)
+        for o in range(NT):
+            mm2(o, 1)
+        w_pair(0, 1, 2)
+        h_centre(0, 2)
+        h_centre(1, 2)
+        outp(0, 1, "S")
+        outp(1, 1, "S")
+        x_quant(4)
+        for t in range(NT):
+            mm1(t, 4)
+        w_pair(2, 3, 2)
+        h_centre(2, 2)
+        h_centre(3, 2)
+        outp(2, 1, "S")
+        outp(3, 1, "S")
+        h_pair(0, 1, 2)
+        d_centre(0, 4)
+        d_centre(1, 4)
+        h_pair(2, 3, 2)
+        d_centre(2, 4)
+        d_centre(3, 4)
+        y_regroup(2, "G")
+
+        d_pair(0, 1, 4)
+        w_centre(0, 3)
+        w_centre(1, 3)
+        d_pair(2, 3, 4)
+        w_centre(2, 3)
+        w_centre(3, 3)
+        y_quant(2)
+        for o in range(NT):
+            mm2(o, 2)
+        w_pair(0, 1, 3)
+        h_centre(0, 3)
+        h_centre(1, 3)
+        h_centre(0, 4)
+        h_centre(1, 4)
+        outp(0, 2, "S")
+        outp(1, 2, "S")
+        w_pair(2, 3, 3)
+        h_centre(2, 3)
+        h_centre(3, 3)
+        h_centre(2, 4)
+        h_centre(3, 4)
+        outp(2, 2, "S")
+        outp(3, 2, "S")
+        for t in range(NT):
+            h_side(t, 3, 0)
+        y_regroup(3, "S")
+        for t in range(NT):
+            h_centre(t, 5)
+        h_pair(0, 1, 4)
+        h_pair(2, 3, 4)
+        y_quant(3)
+        for o in range(NT):
+            mm2(o, 3)
+        y_regroup(4, "S")
+        for o in range(NT):
+            outp(o, 3, "S")
+        h_pair(0, 1, 5)
+        y_quant(4)
+        for o in range(NT):
+            mm2(o, 4)
+        for o in range(NT):
+            outp(o, 4, "S")
+        h_pair(2, 3, 5)
+        y_regroup(5, "V")
+        y_quant(5)
+        for o in range(NT):
+            mm2(o, 5)
+        outp(0, 5, "V")
+        outp(1, 5, "S")
+        outp(2, 5, "V")
+        outp(3, 5, "S")

@@ -25,6 +25,8 @@ KW = 3
 KD = 6
 KB = 9
 NSMALL = 10
+TPE = 0
+TV = (1, 2, 3)
 
 FLOPS = 2 * 2 * 512 * 512 * NPOS + 2 * 9 * 512 * NPOS
 
@@ -53,6 +55,8 @@ def tile_lowrankconv3d_kernel(tc, x, U_kh, U_kw, U_kd, U_c_in, U_c_out, bias, ou
         warm = keep.tile([P, 8], F32, name="warm")
         warm2 = keep.tile([P, 8], F32, name="warm2")
         ident = keep.tile([P, P], BF16, name="ident")
+        ident32 = keep.tile([P, P], F32, name="ident32")
+        diag = [keep.tile([P, P], F32, name="diag%d" % k) for k in range(3)]
         taps = keep.tile([P, NT, NSMALL], F32, name="taps")
         uin_raw = keep.tile([P, PACK, 512], BF16, name="uin_raw")
         uin_g = keep.tile([P, 512, PACK], BF16, name="uin_g", align_bytes=64)
@@ -75,6 +79,7 @@ def tile_lowrankconv3d_kernel(tc, x, U_kh, U_kw, U_kd, U_c_in, U_c_out, bias, ou
         yc = {}
         ys = {}
         po = {}
+        ph = {}
 
         def tap(t, k):
             return taps[:, t, k : k + 1]
@@ -172,10 +177,30 @@ def tile_lowrankconv3d_kernel(tc, x, U_kh, U_kw, U_kd, U_c_in, U_c_out, bias, ou
             z[(t, g)] = zpool.tile([P, w], F32, name="z_%d_%d" % (t, g), tag="z")
             nc.scalar.activation(out=z[(t, g)][:], in_=v[t][:, lo : lo + w], func=COPY, scale=tap(t, KH + 1))
 
+        def need_y3(g):
+            if g not in y3:
+                y3[g] = ypool.tile([P, NT, HG[g][1]], BF16, name="y3_%d" % g, tag="y3")
+
+        def h_pe(g):
+            lo, w = HG[g]
+            ph[g] = ps.tile([P, w], F32, name="ph_%d" % g, tag="ps")
+            terms = [(1, lo)]
+            if lo >= SLICE:
+                terms.append((0, lo - SLICE))
+            if lo + w < NPOS:
+                terms.append((2, lo + SLICE))
+            for n, (k, s) in enumerate(terms):
+                nc.tensor.matmul(
+                    out=ph[g][:], lhsT=diag[k][:], rhs=v[TPE][:, s : s + w], start=(n == 0), stop=(n == len(terms) - 1)
+                )
+
+        def ycopy(g):
+            need_y3(g)
+            nc.scalar.copy(out=y3[g][:, TPE, :], in_=ph[g][:])
+
         def h_side(t, g, k):
             lo, w = HG[g]
-            if g not in y3:
-                y3[g] = ypool.tile([P, NT, w], BF16, name="y3_%d" % g, tag="y3")
+            need_y3(g)
             zz = z[(t, g)]
             last = lo + w == NPOS
             if k == 0:
@@ -191,11 +216,10 @@ def tile_lowrankconv3d_kernel(tc, x, U_kh, U_kw, U_kd, U_c_in, U_c_out, bias, ou
                     op0=MULT, op1=ADD,
                 )
 
-        def h_pair(a, b, g):
-            h_side(a, g, 0)
-            h_side(b, g, 0)
-            h_side(a, g, 2)
-            h_side(b, g, 2)
+        def h_triple(g):
+            for k in (0, 2):
+                for t in TV:
+                    h_side(t, g, k)
 
         def y_regroup(g, eng):
             w = HG[g][1]
@@ -230,16 +254,18 @@ def tile_lowrankconv3d_kernel(tc, x, U_kh, U_kw, U_kd, U_c_in, U_c_out, bias, ou
                 nc.scalar.activation(out=ost[:], in_=po[(o, g)][:], func=IDENT, bias=tap(o, KB), scale=1.0)
             nc.sync.dma_start(out=outv[o * P : (o + 1) * P, lo : lo + w], in_=ost[:])
 
-        nc.vector.memset(small[:], 0.0)
+        nc.gpsimd.memset(small[:].bitcast(F32), 0.0)
         nc.vector.memset(warm[:], 0.0)
-        nc.scalar.dma_start(out=small[KD : KD + 3, :], in_=U_kd)
-        nc.scalar.dma_start(out=small[KW : KW + 3, :], in_=U_kw)
-        nc.scalar.dma_start(out=small[KH : KH + 3, :], in_=U_kh)
-        nc.scalar.dma_start(out=small[KB : KB + 1, :], in_=bias.rearrange("(a n) -> a n", a=1))
+        nc.sync.dma_start(out=small[KD : KD + 3, :], in_=U_kd)
+        nc.sync.dma_start(out=small[KW : KW + 3, :], in_=U_kw)
+        nc.sync.dma_start(out=small[KH : KH + 3, :], in_=U_kh)
+        nc.sync.dma_start(out=small[KB : KB + 1, :], in_=bias.rearrange("(a n) -> a n", a=1))
         nc.scalar.activation(out=warm2[:], in_=warm[:], func=COPY, scale=1.0)
         make_identity(nc, ident[:])
+        make_identity(nc, ident32[:])
         nc.sync.dma_start(out=xraw[0][:], in_=xv[:, :, XP[0][0] : XP[0][0] + XP[0][1]])
-        nc.sync.dma_start(out=uin_raw[:], in_=uinv)
+        nc.sync.dma_start(out=uin_raw[:, :, 0:256], in_=uinv[:, :, 0:256])
+        nc.sync.dma_start(out=uin_raw[:, :, 256:512], in_=uinv[:, :, 256:512])
         for i in range(1, len(XP)):
             nc.sync.dma_start(out=xraw[i][:], in_=xv[:, :, XP[i][0] : XP[i][0] + XP[i][1]])
         nc.sync.dma_start(out=uout_raw[:], in_=uoutv)
@@ -253,6 +279,8 @@ def tile_lowrankconv3d_kernel(tc, x, U_kh, U_kw, U_kd, U_c_in, U_c_out, bias, ou
             nc.tensor.transpose(tp[:, t, :], small[:, t * P : (t + 1) * P], ident[:])
         nc.vector.tensor_copy(out=taps[:], in_=tp[:, :, 0:NSMALL])
         quantise(uin_c[:, 0:256], uin_s[:, 0:256], uin_g[:, 0:256, :])
+        for k in range(3):
+            nc.scalar.activation(out=diag[k][:], in_=ident32[:], func=COPY, scale=tap(TPE, KH + k))
         quantise(uin_c[:, 256:512], uin_s[:, 256:512], uin_g[:, 256:512, :])
         x_regroup(1, "V")
         x_quant(1)
@@ -272,20 +300,23 @@ def tile_lowrankconv3d_kernel(tc, x, U_kh, U_kw, U_kd, U_c_in, U_c_out, bias, ou
         w_centre(2, 0)
         w_centre(3, 0)
         x_quant(2)
-        for t in range(NT):
-            mm1(t, 2)
         w_pair(0, 1, 0)
-        h_centre(0, 0)
+        h_pe(0)
         h_centre(1, 0)
+        mm1(0, 2)
+        mm1(1, 2)
         d_centre(0, 2)
         d_centre(1, 2)
         w_pair(2, 3, 0)
         h_centre(2, 0)
         h_centre(3, 0)
+        mm1(2, 2)
+        mm1(3, 2)
         d_centre(2, 2)
         d_centre(3, 2)
-        for t in range(NT):
+        for t in TV:
             h_side(t, 0, 2)
+        ycopy(0)
         x_regroup(3, "S", 0, 256)
         x_regroup(3, "S", 256, 512)
         y_regroup(0, "G")
@@ -300,10 +331,8 @@ def tile_lowrankconv3d_kernel(tc, x, U_kh, U_kw, U_kd, U_c_in, U_c_out, bias, ou
         w_centre(3, 1)
         regroup("S", uout_g[:, 256:512, :], uout_raw[:, :, 256:512])
         y_quant(0)
-        for t in range(NT):
-            mm1(t, 3)
         w_pair(0, 1, 1)
-        h_centre(0, 1)
+        h_pe(1)
         h_centre(1, 1)
         w_pair(2, 3, 1)
         h_centre(2, 1)
@@ -311,12 +340,16 @@ def tile_lowrankconv3d_kernel(tc, x, U_kh, U_kw, U_kd, U_c_in, U_c_out, bias, ou
         quantise(uout_c[:], uout_s[:], uout_g[:])
         for o in range(NT):
             mm2(o, 0)
-        h_pair(0, 1, 1)
+        h_triple(1)
+        mm1(0, 3)
+        mm1(1, 3)
         d_centre(0, 3)
         d_centre(1, 3)
         outp(0, 0, "S")
         outp(1, 0, "S")
-        h_pair(2, 3, 1)
+        ycopy(1)
+        mm1(2, 3)
+        mm1(3, 3)
         d_centre(2, 3)
         d_centre(3, 3)
         outp(2, 0, "S")
@@ -335,22 +368,24 @@ def tile_lowrankconv3d_kernel(tc, x, U_kh, U_kw, U_kd, U_c_in, U_c_out, bias, ou
         for o in range(NT):
             mm2(o, 1)
         w_pair(0, 1, 2)
-        h_centre(0, 2)
+        h_pe(2)
         h_centre(1, 2)
         outp(0, 1, "S")
         outp(1, 1, "S")
         x_quant(4)
-        for t in range(NT):
-            mm1(t, 4)
         w_pair(2, 3, 2)
         h_centre(2, 2)
         h_centre(3, 2)
         outp(2, 1, "S")
         outp(3, 1, "S")
-        h_pair(0, 1, 2)
+        h_triple(2)
+        mm1(0, 4)
+        mm1(1, 4)
         d_centre(0, 4)
         d_centre(1, 4)
-        h_pair(2, 3, 2)
+        ycopy(2)
+        mm1(2, 4)
+        mm1(3, 4)
         d_centre(2, 4)
         d_centre(3, 4)
         y_regroup(2, "G")
@@ -365,9 +400,10 @@ def tile_lowrankconv3d_kernel(tc, x, U_kh, U_kw, U_kd, U_c_in, U_c_out, bias, ou
         for o in range(NT):
             mm2(o, 2)
         w_pair(0, 1, 3)
-        h_centre(0, 3)
+        h_pe(3)
+        h_pe(4)
+        h_pe(5)
         h_centre(1, 3)
-        h_centre(0, 4)
         h_centre(1, 4)
         outp(0, 2, "S")
         outp(1, 2, "S")
@@ -378,26 +414,30 @@ def tile_lowrankconv3d_kernel(tc, x, U_kh, U_kw, U_kd, U_c_in, U_c_out, bias, ou
         h_centre(3, 4)
         outp(2, 2, "S")
         outp(3, 2, "S")
-        for t in range(NT):
+        ycopy(3)
+        for t in TV:
             h_side(t, 3, 0)
         y_regroup(3, "S")
-        for t in range(NT):
+        ycopy(4)
+        for t in TV:
             h_centre(t, 5)
-        h_pair(0, 1, 4)
-        h_pair(2, 3, 4)
+        ycopy(5)
+        h_triple(4)
         y_quant(3)
         for o in range(NT):
             mm2(o, 3)
         y_regroup(4, "S")
         for o in range(NT):
             outp(o, 3, "S")
-        h_pair(0, 1, 5)
+        for t in TV:
+            h_side(t, 5, 0)
         y_quant(4)
         for o in range(NT):
             mm2(o, 4)
         for o in range(NT):
             outp(o, 4, "S")
-        h_pair(2, 3, 5)
+        for t in TV:
+            h_side(t, 5, 2)
         y_regroup(5, "V")
         y_quant(5)
         for o in range(NT):

@@ -45,9 +45,9 @@ def tile_lowrankconv3d_kernel(tc, x, U_kh, U_kw, U_kd, U_c_in, U_c_out, bias, ou
         keep = ctx.enter_context(tc.tile_pool(name="keep", bufs=1))
         xgp = ctx.enter_context(tc.tile_pool(name="xgp", bufs=1))
         upool = ctx.enter_context(tc.tile_pool(name="upool", bufs=8))
-        zpool = ctx.enter_context(tc.tile_pool(name="zpool", bufs=8))
+        zpool = ctx.enter_context(tc.tile_pool(name="zpool", bufs=12))
         ypool = ctx.enter_context(tc.tile_pool(name="ypool", bufs=3))
-        opool = ctx.enter_context(tc.tile_pool(name="opool", bufs=6))
+        opool = ctx.enter_context(tc.tile_pool(name="opool", bufs=12))
         ps = ctx.enter_context(tc.psum_pool(name="ps", bufs=8))
         ctx.enter_context(tc.manual_schedule())
 
@@ -279,10 +279,8 @@ def tile_lowrankconv3d_kernel(tc, x, U_kh, U_kw, U_kd, U_c_in, U_c_out, bias, ou
             nc.tensor.transpose(tp[:, t, :], small[:, t * P : (t + 1) * P], ident[:])
         nc.vector.tensor_copy(out=taps[:], in_=tp[:, :, 0:NSMALL])
         quantise(uin_c[:, 0:256], uin_s[:, 0:256], uin_g[:, 0:256, :])
-        for k in range(3):
-            nc.scalar.activation(out=diag[k][:], in_=ident32[:], func=COPY, scale=tap(TPE, KH + k))
-        quantise(uin_c[:, 256:512], uin_s[:, 256:512], uin_g[:, 256:512, :])
         x_regroup(1, "V")
+        quantise(uin_c[:, 256:512], uin_s[:, 256:512], uin_g[:, 256:512, :])
         x_quant(1)
         for i in (0, 1):
             for t in range(NT):
@@ -293,6 +291,8 @@ def tile_lowrankconv3d_kernel(tc, x, U_kh, U_kw, U_kd, U_c_in, U_c_out, bias, ou
 
         d_pair(0, 1, 0)
         d_pair(2, 3, 0)
+        for k in range(3):
+            nc.scalar.activation(out=diag[k][:], in_=ident32[:], func=COPY, scale=tap(TPE, KH + k))
         d_pair(0, 1, 1)
         w_centre(0, 0)
         w_centre(1, 0)
@@ -300,18 +300,16 @@ def tile_lowrankconv3d_kernel(tc, x, U_kh, U_kw, U_kd, U_c_in, U_c_out, bias, ou
         w_centre(2, 0)
         w_centre(3, 0)
         x_quant(2)
+        for t in range(NT):
+            mm1(t, 2)
         w_pair(0, 1, 0)
         h_pe(0)
         h_centre(1, 0)
-        mm1(0, 2)
-        mm1(1, 2)
         d_centre(0, 2)
         d_centre(1, 2)
         w_pair(2, 3, 0)
         h_centre(2, 0)
         h_centre(3, 0)
-        mm1(2, 2)
-        mm1(3, 2)
         d_centre(2, 2)
         d_centre(3, 2)
         for t in TV:
@@ -325,74 +323,71 @@ def tile_lowrankconv3d_kernel(tc, x, U_kh, U_kw, U_kd, U_c_in, U_c_out, bias, ou
         w_centre(0, 1)
         w_centre(1, 1)
         regroup("S", uout_g[:, 0:256, :], uout_raw[:, :, 0:256])
-        x_quant(3)
         d_pair(2, 3, 2)
         w_centre(2, 1)
         w_centre(3, 1)
         regroup("S", uout_g[:, 256:512, :], uout_raw[:, :, 256:512])
+        x_quant(3)
         y_quant(0)
+        for t in range(NT):
+            mm1(t, 3)
         w_pair(0, 1, 1)
         h_pe(1)
         h_centre(1, 1)
+        x_regroup(4, "S", 0, 256)
         w_pair(2, 3, 1)
         h_centre(2, 1)
         h_centre(3, 1)
         quantise(uout_c[:], uout_s[:], uout_g[:])
-        for o in range(NT):
-            mm2(o, 0)
         h_triple(1)
-        mm1(0, 3)
-        mm1(1, 3)
         d_centre(0, 3)
         d_centre(1, 3)
-        outp(0, 0, "S")
-        outp(1, 0, "S")
         ycopy(1)
-        mm1(2, 3)
-        mm1(3, 3)
         d_centre(2, 3)
         d_centre(3, 3)
-        outp(2, 0, "S")
-        outp(3, 0, "S")
         y_regroup(1, "G")
+        for o in range(NT):
+            mm2(o, 0)
 
         d_pair(0, 1, 3)
         w_centre(0, 2)
         w_centre(1, 2)
-        x_regroup(4, "S", 0, 256)
+        x_regroup(4, "S", 256, 512)
+        outp(0, 0, "S")
         d_pair(2, 3, 3)
         w_centre(2, 2)
         w_centre(3, 2)
-        x_regroup(4, "S", 256, 512)
+        outp(1, 0, "S")
+        outp(2, 0, "S")
+        outp(3, 0, "S")
+        x_quant(4)
         y_quant(1)
-        for o in range(NT):
+        for t in range(NT):
+            mm1(t, 4)
+        for o in range(3):
             mm2(o, 1)
         w_pair(0, 1, 2)
         h_pe(2)
         h_centre(1, 2)
         outp(0, 1, "S")
+        mm2(3, 1)
         outp(1, 1, "S")
-        x_quant(4)
         w_pair(2, 3, 2)
         h_centre(2, 2)
         h_centre(3, 2)
-        outp(2, 1, "S")
-        outp(3, 1, "S")
         h_triple(2)
-        mm1(0, 4)
-        mm1(1, 4)
         d_centre(0, 4)
         d_centre(1, 4)
         ycopy(2)
-        mm1(2, 4)
-        mm1(3, 4)
         d_centre(2, 4)
         d_centre(3, 4)
         y_regroup(2, "G")
 
         d_pair(0, 1, 4)
+        outp(2, 1, "S")
         w_centre(0, 3)
         w_centre(1, 3)
+        outp(3, 1, "S")
         d_pair(2, 3, 4)
         w_centre(2, 3)
         w_centre(3, 3)
@@ -407,41 +402,44 @@ def tile_lowrankconv3d_kernel(tc, x, U_kh, U_kw, U_kd, U_c_in, U_c_out, bias, ou
         h_centre(1, 4)
         outp(0, 2, "S")
         outp(1, 2, "S")
+        h_centre(1, 5)
         w_pair(2, 3, 3)
         h_centre(2, 3)
         h_centre(3, 3)
+        ycopy(3)
         h_centre(2, 4)
         h_centre(3, 4)
-        outp(2, 2, "S")
-        outp(3, 2, "S")
-        ycopy(3)
+        ycopy(4)
         for t in TV:
             h_side(t, 3, 0)
         y_regroup(3, "S")
-        ycopy(4)
-        for t in TV:
-            h_centre(t, 5)
+        h_centre(2, 5)
+        h_centre(3, 5)
         ycopy(5)
         h_triple(4)
+        y_regroup(4, "V")
         y_quant(3)
         for o in range(NT):
             mm2(o, 3)
-        y_regroup(4, "S")
-        for o in range(NT):
-            outp(o, 3, "S")
+        outp(2, 2, "S")
+        outp(3, 2, "S")
         for t in TV:
             h_side(t, 5, 0)
         y_quant(4)
         for o in range(NT):
             mm2(o, 4)
         for o in range(NT):
-            outp(o, 4, "S")
+            outp(o, 3, "S")
         for t in TV:
             h_side(t, 5, 2)
         y_regroup(5, "V")
+        outp(0, 4, "V")
         y_quant(5)
         for o in range(NT):
             mm2(o, 5)
+        outp(1, 4, "S")
+        outp(2, 4, "V")
+        outp(3, 4, "S")
         outp(0, 5, "V")
         outp(1, 5, "S")
         outp(2, 5, "V")

@@ -49,7 +49,6 @@ def tile_lowrankconv3d_kernel(tc, x, U_kh, U_kw, U_kd, U_c_in, U_c_out, bias, ou
         ypool = ctx.enter_context(tc.tile_pool(name="ypool", bufs=3))
         opool = ctx.enter_context(tc.tile_pool(name="opool", bufs=12))
         ps = ctx.enter_context(tc.psum_pool(name="ps", bufs=8))
-        ctx.enter_context(tc.manual_schedule())
 
         small = keep.tile([P, 512], BF16, name="small")
         warm = keep.tile([P, 8], F32, name="warm")
@@ -256,15 +255,15 @@ def tile_lowrankconv3d_kernel(tc, x, U_kh, U_kw, U_kd, U_c_in, U_c_out, bias, ou
 
         nc.gpsimd.memset(small[:].bitcast(F32), 0.0)
         nc.vector.memset(warm[:], 0.0)
-        nc.sync.dma_start(out=small[KD : KD + 3, :], in_=U_kd)
-        nc.sync.dma_start(out=small[KW : KW + 3, :], in_=U_kw)
-        nc.sync.dma_start(out=small[KH : KH + 3, :], in_=U_kh)
-        nc.sync.dma_start(out=small[KB : KB + 1, :], in_=bias.rearrange("(a n) -> a n", a=1))
         nc.scalar.activation(out=warm2[:], in_=warm[:], func=COPY, scale=1.0)
         make_identity(nc, ident[:])
         make_identity(nc, ident32[:])
         nc.sync.dma_start(out=xraw[0][:], in_=xv[:, :, XP[0][0] : XP[0][0] + XP[0][1]])
         nc.sync.dma_start(out=uin_raw[:, :, 0:256], in_=uinv[:, :, 0:256])
+        nc.sync.dma_start(out=small[KD : KD + 3, :], in_=U_kd)
+        nc.sync.dma_start(out=small[KW : KW + 3, :], in_=U_kw)
+        nc.sync.dma_start(out=small[KH : KH + 3, :], in_=U_kh)
+        nc.sync.dma_start(out=small[KB : KB + 1, :], in_=bias.rearrange("(a n) -> a n", a=1))
         nc.sync.dma_start(out=uin_raw[:, :, 256:512], in_=uinv[:, :, 256:512])
         for i in range(1, len(XP)):
             nc.sync.dma_start(out=xraw[i][:], in_=xv[:, :, XP[i][0] : XP[i][0] + XP[i][1]])

@@ -49,6 +49,7 @@ def tile_lowrankconv3d_kernel(tc, x, U_kh, U_kw, U_kd, U_c_in, U_c_out, bias, ou
         ypool = ctx.enter_context(tc.tile_pool(name="ypool", bufs=3))
         opool = ctx.enter_context(tc.tile_pool(name="opool", bufs=12))
         ps = ctx.enter_context(tc.psum_pool(name="ps", bufs=8))
+        ctx.enter_context(tc.manual_schedule())
 
         small = keep.tile([P, 512], BF16, name="small")
         warm = keep.tile([P, 8], F32, name="warm")

@@ -256,15 +256,15 @@ def tile_lowrankconv3d_kernel(tc, x, U_kh, U_kw, U_kd, U_c_in, U_c_out, bias, ou
 
         nc.gpsimd.memset(small[:].bitcast(F32), 0.0)
         nc.vector.memset(warm[:], 0.0)
+        nc.scalar.dma_start(out=small[KD : KD + 3, :], in_=U_kd)
+        nc.scalar.dma_start(out=small[KW : KW + 3, :], in_=U_kw)
+        nc.scalar.dma_start(out=small[KH : KH + 3, :], in_=U_kh)
+        nc.scalar.dma_start(out=small[KB : KB + 1, :], in_=bias.rearrange("(a n) -> a n", a=1))
         nc.scalar.activation(out=warm2[:], in_=warm[:], func=COPY, scale=1.0)
         make_identity(nc, ident[:])
         make_identity(nc, ident32[:])
         nc.sync.dma_start(out=xraw[0][:], in_=xv[:, :, XP[0][0] : XP[0][0] + XP[0][1]])
         nc.sync.dma_start(out=uin_raw[:, :, 0:256], in_=uinv[:, :, 0:256])
-        nc.sync.dma_start(out=small[KD : KD + 3, :], in_=U_kd)
-        nc.sync.dma_start(out=small[KW : KW + 3, :], in_=U_kw)
-        nc.sync.dma_start(out=small[KH : KH + 3, :], in_=U_kh)
-        nc.sync.dma_start(out=small[KB : KB + 1, :], in_=bias.rearrange("(a n) -> a n", a=1))
         nc.sync.dma_start(out=uin_raw[:, :, 256:512], in_=uinv[:, :, 256:512])
         for i in range(1, len(XP)):
             nc.sync.dma_start(out=xraw[i][:], in_=xv[:, :, XP[i][0] : XP[i][0] + XP[i][1]])
@@ -277,8 +277,8 @@ def tile_lowrankconv3d_kernel(tc, x, U_kh, U_kw, U_kd, U_c_in, U_c_out, bias, ou
         tp = ps.tile([P, NT, P], BF16, name="tp", tag="ps")
         for t in range(NT):
             nc.tensor.transpose(tp[:, t, :], small[:, t * P : (t + 1) * P], ident[:])
-        nc.vector.tensor_copy(out=taps[:], in_=tp[:, :, 0:NSMALL])
         quantise(uin_c[:, 0:256], uin_s[:, 0:256], uin_g[:, 0:256, :])
+        nc.vector.tensor_copy(out=taps[:], in_=tp[:, :, 0:NSMALL])
         x_regroup(1, "V")
         quantise(uin_c[:, 256:512], uin_s[:, 256:512], uin_g[:, 256:512, :])
         x_quant(1)
@@ -335,11 +335,19 @@ def tile_lowrankconv3d_kernel(tc, x, U_kh, U_kw, U_kd, U_c_in, U_c_out, bias, ou
         h_pe(1)
         h_centre(1, 1)
         x_regroup(4, "S", 0, 256)
-        w_pair(2, 3, 1)
+        w_side(2, 1, 0)
+        w_side(3, 1, 0)
+        h_side(1, 1, 0)
+        w_side(2, 1, 2)
+        w_side(3, 1, 2)
         h_centre(2, 1)
         h_centre(3, 1)
         quantise(uout_c[:], uout_s[:], uout_g[:])
-        h_triple(1)
+        h_side(1, 1, 2)
+        h_side(2, 1, 0)
+        h_side(3, 1, 0)
+        h_side(2, 1, 2)
+        h_side(3, 1, 2)
         d_centre(0, 3)
         d_centre(1, 3)
         ycopy(1)
@@ -360,8 +368,8 @@ def tile_lowrankconv3d_kernel(tc, x, U_kh, U_kw, U_kd, U_c_in, U_c_out, bias, ou
         outp(1, 0, "S")
         outp(2, 0, "S")
         outp(3, 0, "S")
-        x_quant(4)
         y_quant(1)
+        x_quant(4)
         for t in range(NT):
             mm1(t, 4)
         for o in range(3):
@@ -372,10 +380,18 @@ def tile_lowrankconv3d_kernel(tc, x, U_kh, U_kw, U_kd, U_c_in, U_c_out, bias, ou
         outp(0, 1, "S")
         mm2(3, 1)
         outp(1, 1, "S")
-        w_pair(2, 3, 2)
+        w_side(2, 2, 0)
+        w_side(3, 2, 0)
+        h_side(1, 2, 0)
+        w_side(2, 2, 2)
+        w_side(3, 2, 2)
         h_centre(2, 2)
         h_centre(3, 2)
-        h_triple(2)
+        h_side(1, 2, 2)
+        h_side(2, 2, 0)
+        h_side(3, 2, 0)
+        h_side(2, 2, 2)
+        h_side(3, 2, 2)
         d_centre(0, 4)
         d_centre(1, 4)
         ycopy(2)
@@ -403,20 +419,29 @@ def tile_lowrankconv3d_kernel(tc, x, U_kh, U_kw, U_kd, U_c_in, U_c_out, bias, ou
         outp(0, 2, "S")
         outp(1, 2, "S")
         h_centre(1, 5)
-        w_pair(2, 3, 3)
+        w_side(2, 3, 0)
+        w_side(3, 3, 0)
+        h_side(1, 3, 0)
+        w_side(2, 3, 2)
+        w_side(3, 3, 2)
         h_centre(2, 3)
         h_centre(3, 3)
         ycopy(3)
         h_centre(2, 4)
         h_centre(3, 4)
         ycopy(4)
-        for t in TV:
-            h_side(t, 3, 0)
+        h_side(1, 4, 0)
+        h_side(2, 3, 0)
+        h_side(3, 3, 0)
         y_regroup(3, "S")
         h_centre(2, 5)
         h_centre(3, 5)
         ycopy(5)
-        h_triple(4)
+        h_side(1, 4, 2)
+        h_side(2, 4, 0)
+        h_side(3, 4, 0)
+        h_side(2, 4, 2)
+        h_side(3, 4, 2)
         y_regroup(4, "V")
         y_quant(3)
         for o in range(NT):

@@ -256,15 +256,15 @@ def tile_lowrankconv3d_kernel(tc, x, U_kh, U_kw, U_kd, U_c_in, U_c_out, bias, ou
 
         nc.gpsimd.memset(small[:].bitcast(F32), 0.0)
         nc.vector.memset(warm[:], 0.0)
-        nc.scalar.dma_start(out=small[KD : KD + 3, :], in_=U_kd)
-        nc.scalar.dma_start(out=small[KW : KW + 3, :], in_=U_kw)
-        nc.scalar.dma_start(out=small[KH : KH + 3, :], in_=U_kh)
-        nc.scalar.dma_start(out=small[KB : KB + 1, :], in_=bias.rearrange("(a n) -> a n", a=1))
         nc.scalar.activation(out=warm2[:], in_=warm[:], func=COPY, scale=1.0)
         make_identity(nc, ident[:])
         make_identity(nc, ident32[:])
         nc.sync.dma_start(out=xraw[0][:], in_=xv[:, :, XP[0][0] : XP[0][0] + XP[0][1]])
         nc.sync.dma_start(out=uin_raw[:, :, 0:256], in_=uinv[:, :, 0:256])
+        nc.sync.dma_start(out=small[KD : KD + 3, :], in_=U_kd)
+        nc.sync.dma_start(out=small[KW : KW + 3, :], in_=U_kw)
+        nc.sync.dma_start(out=small[KH : KH + 3, :], in_=U_kh)
+        nc.sync.dma_start(out=small[KB : KB + 1, :], in_=bias.rearrange("(a n) -> a n", a=1))
         nc.sync.dma_start(out=uin_raw[:, :, 256:512], in_=uinv[:, :, 256:512])
         for i in range(1, len(XP)):
             nc.sync.dma_start(out=xraw[i][:], in_=xv[:, :, XP[i][0] : XP[i][0] + XP[i][1]])
@@ -277,8 +277,8 @@ def tile_lowrankconv3d_kernel(tc, x, U_kh, U_kw, U_kd, U_c_in, U_c_out, bias, ou
         tp = ps.tile([P, NT, P], BF16, name="tp", tag="ps")
         for t in range(NT):
             nc.tensor.transpose(tp[:, t, :], small[:, t * P : (t + 1) * P], ident[:])
-        quantise(uin_c[:, 0:256], uin_s[:, 0:256], uin_g[:, 0:256, :])
         nc.vector.tensor_copy(out=taps[:], in_=tp[:, :, 0:NSMALL])
+        quantise(uin_c[:, 0:256], uin_s[:, 0:256], uin_g[:, 0:256, :])
         x_regroup(1, "V")
         quantise(uin_c[:, 256:512], uin_s[:, 256:512], uin_g[:, 256:512, :])
         x_quant(1)
@@ -287,7 +287,7 @@ def tile_lowrankconv3d_kernel(tc, x, U_kh, U_kw, U_kd, U_c_in, U_c_out, bias, ou
                 mm1(t, i)
             for t in range(NT):
                 d_centre(t, i)
-        x_regroup(2, "G")
+        x_regroup(2, "S")
 
         d_pair(0, 1, 0)
         d_pair(2, 3, 0)
@@ -317,7 +317,7 @@ def tile_lowrankconv3d_kernel(tc, x, U_kh, U_kw, U_kd, U_c_in, U_c_out, bias, ou
         ycopy(0)
         x_regroup(3, "S", 0, 256)
         x_regroup(3, "S", 256, 512)
-        y_regroup(0, "G")
+        y_regroup(0, "S")
 
         d_pair(0, 1, 2)
         w_centre(0, 1)
@@ -335,25 +335,17 @@ def tile_lowrankconv3d_kernel(tc, x, U_kh, U_kw, U_kd, U_c_in, U_c_out, bias, ou
         h_pe(1)
         h_centre(1, 1)
         x_regroup(4, "S", 0, 256)
-        w_side(2, 1, 0)
-        w_side(3, 1, 0)
-        h_side(1, 1, 0)
-        w_side(2, 1, 2)
-        w_side(3, 1, 2)
+        w_pair(2, 3, 1)
         h_centre(2, 1)
         h_centre(3, 1)
         quantise(uout_c[:], uout_s[:], uout_g[:])
-        h_side(1, 1, 2)
-        h_side(2, 1, 0)
-        h_side(3, 1, 0)
-        h_side(2, 1, 2)
-        h_side(3, 1, 2)
+        h_triple(1)
         d_centre(0, 3)
         d_centre(1, 3)
         ycopy(1)
         d_centre(2, 3)
         d_centre(3, 3)
-        y_regroup(1, "G")
+        y_regroup(1, "S")
         for o in range(NT):
             mm2(o, 0)
 
@@ -368,8 +360,8 @@ def tile_lowrankconv3d_kernel(tc, x, U_kh, U_kw, U_kd, U_c_in, U_c_out, bias, ou
         outp(1, 0, "S")
         outp(2, 0, "S")
         outp(3, 0, "S")
-        y_quant(1)
         x_quant(4)
+        y_quant(1)
         for t in range(NT):
             mm1(t, 4)
         for o in range(3):
@@ -380,24 +372,16 @@ def tile_lowrankconv3d_kernel(tc, x, U_kh, U_kw, U_kd, U_c_in, U_c_out, bias, ou
         outp(0, 1, "S")
         mm2(3, 1)
         outp(1, 1, "S")
-        w_side(2, 2, 0)
-        w_side(3, 2, 0)
-        h_side(1, 2, 0)
-        w_side(2, 2, 2)
-        w_side(3, 2, 2)
+        w_pair(2, 3, 2)
         h_centre(2, 2)
         h_centre(3, 2)
-        h_side(1, 2, 2)
-        h_side(2, 2, 0)
-        h_side(3, 2, 0)
-        h_side(2, 2, 2)
-        h_side(3, 2, 2)
+        h_triple(2)
         d_centre(0, 4)
         d_centre(1, 4)
         ycopy(2)
         d_centre(2, 4)
         d_centre(3, 4)
-        y_regroup(2, "G")
+        y_regroup(2, "S")
 
         d_pair(0, 1, 4)
         outp(2, 1, "S")
@@ -419,29 +403,20 @@ def tile_lowrankconv3d_kernel(tc, x, U_kh, U_kw, U_kd, U_c_in, U_c_out, bias, ou
         outp(0, 2, "S")
         outp(1, 2, "S")
         h_centre(1, 5)
-        w_side(2, 3, 0)
-        w_side(3, 3, 0)
-        h_side(1, 3, 0)
-        w_side(2, 3, 2)
-        w_side(3, 3, 2)
+        w_pair(2, 3, 3)
         h_centre(2, 3)
         h_centre(3, 3)
         ycopy(3)
         h_centre(2, 4)
         h_centre(3, 4)
         ycopy(4)
-        h_side(1, 4, 0)
-        h_side(2, 3, 0)
-        h_side(3, 3, 0)
+        for t in TV:
+            h_side(t, 3, 0)
         y_regroup(3, "S")
         h_centre(2, 5)
         h_centre(3, 5)
         ycopy(5)
-        h_side(1, 4, 2)
-        h_side(2, 4, 0)
-        h_side(3, 4, 0)
-        h_side(2, 4, 2)
-        h_side(3, 4, 2)
+        h_triple(4)
         y_regroup(4, "V")
         y_quant(3)
         for o in range(NT):

@@ -80,6 +80,8 @@ def tile_lowrankconv3d_kernel(tc, x, U_kh, U_kw, U_kd, U_c_in, U_c_out, bias, ou
         ys = {}
         po = {}
         ph = {}
+        p0 = {}
+        p2 = {}
 
         def tap(t, k):
             return taps[:, t, k : k + 1]
@@ -216,6 +218,26 @@ def tile_lowrankconv3d_kernel(tc, x, U_kh, U_kw, U_kd, U_c_in, U_c_out, bias, ou
                     op0=MULT, op1=ADD,
                 )
 
+        def h_scale(t, g):
+            lo, w = HG[g]
+            if lo >= SLICE:
+                p0[g] = zpool.tile([P, w], F32, name="p0_%d" % g, tag="p")
+                nc.scalar.activation(out=p0[g][:], in_=v[t][:, lo - SLICE : lo + w - SLICE], func=COPY, scale=tap(t, KH))
+            p2[g] = zpool.tile([P, w], F32, name="p2_%d" % g, tag="p")
+            nc.scalar.activation(out=p2[g][:], in_=v[t][:, lo + SLICE : lo + w + SLICE], func=COPY, scale=tap(t, KH + 2))
+
+        def h_centre_late(t, g, told):
+            lo, w = HG[g]
+            z[(t, g)] = z[(told, g)]
+            nc.scalar.activation(out=z[(t, g)][:], in_=v[t][:, lo : lo + w], func=COPY, scale=tap(t, KH + 1))
+
+        def h_add(t, g):
+            lo, w = HG[g]
+            zz = z[(t, g)]
+            if lo >= SLICE:
+                nc.gpsimd.tensor_tensor(out=zz[:], in0=zz[:], in1=p0[g][:], op=ADD)
+            nc.gpsimd.tensor_tensor(out=y3[g][:, t, :], in0=zz[:], in1=p2[g][:], op=ADD)
+
         def h_triple(g):
             for k in (0, 2):
                 for t in TV:
@@ -287,7 +309,7 @@ def tile_lowrankconv3d_kernel(tc, x, U_kh, U_kw, U_kd, U_c_in, U_c_out, bias, ou
                 mm1(t, i)
             for t in range(NT):
                 d_centre(t, i)
-        x_regroup(2, "S")
+        x_regroup(2, "G")
 
         d_pair(0, 1, 0)
         d_pair(2, 3, 0)
@@ -309,15 +331,17 @@ def tile_lowrankconv3d_kernel(tc, x, U_kh, U_kw, U_kd, U_c_in, U_c_out, bias, ou
         d_centre(1, 2)
         w_pair(2, 3, 0)
         h_centre(2, 0)
-        h_centre(3, 0)
+        h_scale(3, 0)
         d_centre(2, 2)
         d_centre(3, 2)
-        for t in TV:
-            h_side(t, 0, 2)
+        h_side(1, 0, 2)
+        h_side(2, 0, 2)
+        h_centre_late(3, 0, 1)
+        h_add(3, 0)
         ycopy(0)
         x_regroup(3, "S", 0, 256)
         x_regroup(3, "S", 256, 512)
-        y_regroup(0, "S")
+        y_regroup(0, "G")
 
         d_pair(0, 1, 2)
         w_centre(0, 1)
@@ -334,18 +358,22 @@ def tile_lowrankconv3d_kernel(tc, x, U_kh, U_kw, U_kd, U_c_in, U_c_out, bias, ou
         w_pair(0, 1, 1)
         h_pe(1)
         h_centre(1, 1)
-        x_regroup(4, "S", 0, 256)
-        w_pair(2, 3, 1)
-        h_centre(2, 1)
-        h_centre(3, 1)
-        quantise(uout_c[:], uout_s[:], uout_g[:])
-        h_triple(1)
         d_centre(0, 3)
         d_centre(1, 3)
-        ycopy(1)
+        w_pair(2, 3, 1)
+        h_centre(2, 1)
+        h_scale(3, 1)
+        quantise(uout_c[:], uout_s[:], uout_g[:])
+        h_side(1, 1, 0)
+        h_side(2, 1, 0)
+        h_side(1, 1, 2)
+        h_side(2, 1, 2)
         d_centre(2, 3)
+        h_centre_late(3, 1, 1)
+        h_add(3, 1)
         d_centre(3, 3)
-        y_regroup(1, "S")
+        ycopy(1)
+        x_regroup(4, "S", 0, 256)
         for o in range(NT):
             mm2(o, 0)
 
@@ -358,30 +386,31 @@ def tile_lowrankconv3d_kernel(tc, x, U_kh, U_kw, U_kd, U_c_in, U_c_out, bias, ou
         w_centre(2, 2)
         w_centre(3, 2)
         outp(1, 0, "S")
+        y_regroup(1, "S")
         outp(2, 0, "S")
         outp(3, 0, "S")
         x_quant(4)
-        y_quant(1)
         for t in range(NT):
             mm1(t, 4)
-        for o in range(3):
-            mm2(o, 1)
         w_pair(0, 1, 2)
         h_pe(2)
         h_centre(1, 2)
-        outp(0, 1, "S")
-        mm2(3, 1)
-        outp(1, 1, "S")
         w_pair(2, 3, 2)
+        y_quant(1)
+        for o in range(3):
+            mm2(o, 1)
         h_centre(2, 2)
         h_centre(3, 2)
         h_triple(2)
+        outp(0, 1, "S")
+        mm2(3, 1)
         d_centre(0, 4)
         d_centre(1, 4)
         ycopy(2)
         d_centre(2, 4)
         d_centre(3, 4)
-        y_regroup(2, "S")
+        outp(1, 1, "S")
+        y_regroup(2, "G")
 
         d_pair(0, 1, 4)
         outp(2, 1, "S")

@@ -22,9 +22,9 @@ CHUNK = 512
 NT = 4
 KH = 0
 KW = 3
-KD = 6
-KB = 9
-NSMALL = 10
+KB = 6
+NSMALL = 7
+KD = 7
 TPE = 0
 TV = (1, 2, 3)
 
@@ -51,12 +51,14 @@ def tile_lowrankconv3d_kernel(tc, x, U_kh, U_kw, U_kd, U_c_in, U_c_out, bias, ou
         ps = ctx.enter_context(tc.psum_pool(name="ps", bufs=8))
         ctx.enter_context(tc.manual_schedule())
 
+        smalld = keep.tile([P, 512], BF16, name="smalld")
         small = keep.tile([P, 512], BF16, name="small")
         warm = keep.tile([P, 8], F32, name="warm")
         warm2 = keep.tile([P, 8], F32, name="warm2")
         ident = keep.tile([P, P], BF16, name="ident")
         ident32 = keep.tile([P, P], F32, name="ident32")
         diag = [keep.tile([P, P], F32, name="diag%d" % k) for k in range(3)]
+        tapsd = keep.tile([P, NT, 3], F32, name="tapsd")
         taps = keep.tile([P, NT, NSMALL], F32, name="taps")
         uin_raw = keep.tile([P, PACK, 512], BF16, name="uin_raw")
         uin_g = keep.tile([P, 512, PACK], BF16, name="uin_g", align_bytes=64)
@@ -84,6 +86,8 @@ def tile_lowrankconv3d_kernel(tc, x, U_kh, U_kw, U_kd, U_c_in, U_c_out, bias, ou
         p2 = {}
 
         def tap(t, k):
+            if k >= KD:
+                return tapsd[:, t, k - KD : k - KD + 1]
             return taps[:, t, k : k + 1]
 
         def regroup(eng, dst, src):
@@ -276,6 +280,7 @@ def tile_lowrankconv3d_kernel(tc, x, U_kh, U_kw, U_kd, U_c_in, U_c_out, bias, ou
                 nc.scalar.activation(out=ost[:], in_=po[(o, g)][:], func=IDENT, bias=tap(o, KB), scale=1.0)
             nc.sync.dma_start(out=outv[o * P : (o + 1) * P, lo : lo + w], in_=ost[:])
 
+        nc.gpsimd.memset(smalld[:].bitcast(F32), 0.0)
         nc.gpsimd.memset(small[:].bitcast(F32), 0.0)
         nc.vector.memset(warm[:], 0.0)
         nc.scalar.activation(out=warm2[:], in_=warm[:], func=COPY, scale=1.0)
@@ -283,32 +288,44 @@ def tile_lowrankconv3d_kernel(tc, x, U_kh, U_kw, U_kd, U_c_in, U_c_out, bias, ou
         make_identity(nc, ident32[:])
         nc.sync.dma_start(out=xraw[0][:], in_=xv[:, :, XP[0][0] : XP[0][0] + XP[0][1]])
         nc.sync.dma_start(out=uin_raw[:, :, 0:256], in_=uinv[:, :, 0:256])
-        nc.sync.dma_start(out=small[KD : KD + 3, :], in_=U_kd)
+        nc.sync.dma_start(out=smalld[0:3, :], in_=U_kd)
+        nc.sync.dma_start(out=uin_raw[:, :, 256:512], in_=uinv[:, :, 256:512])
+        nc.sync.dma_start(out=xraw[1][:], in_=xv[:, :, XP[1][0] : XP[1][0] + XP[1][1]])
         nc.sync.dma_start(out=small[KW : KW + 3, :], in_=U_kw)
         nc.sync.dma_start(out=small[KH : KH + 3, :], in_=U_kh)
         nc.sync.dma_start(out=small[KB : KB + 1, :], in_=bias.rearrange("(a n) -> a n", a=1))
-        nc.sync.dma_start(out=uin_raw[:, :, 256:512], in_=uinv[:, :, 256:512])
-        for i in range(1, len(XP)):
+        for i in range(2, len(XP)):
             nc.sync.dma_start(out=xraw[i][:], in_=xv[:, :, XP[i][0] : XP[i][0] + XP[i][1]])
         nc.sync.dma_start(out=uout_raw[:], in_=uoutv)
+
+        def spread(dst, src, n, name):
+            tp = ps.tile([P, NT, P], BF16, name=name, tag="ps")
+            for t in range(NT):
+                nc.tensor.transpose(tp[:, t, :], src[:, t * P : (t + 1) * P], ident[:])
+            nc.scalar.copy(out=dst[:], in_=tp[:, :, 0:n])
 
         x_regroup(0, "V")
         x_quant(0)
         regroup("V", uin_g[:, 0:256, :], uin_raw[:, :, 0:256])
+        spread(tapsd, smalld, 3, "tpd")
         regroup("S", uin_g[:, 256:512, :], uin_raw[:, :, 256:512])
-        tp = ps.tile([P, NT, P], BF16, name="tp", tag="ps")
-        for t in range(NT):
-            nc.tensor.transpose(tp[:, t, :], small[:, t * P : (t + 1) * P], ident[:])
-        nc.vector.tensor_copy(out=taps[:], in_=tp[:, :, 0:NSMALL])
         quantise(uin_c[:, 0:256], uin_s[:, 0:256], uin_g[:, 0:256, :])
         x_regroup(1, "V")
-        quantise(uin_c[:, 256:512], uin_s[:, 256:512], uin_g[:, 256:512, :])
+        for t in (0, 1):
+            mm1(t, 0)
+        for t in (0, 1):
+            d_centre(t, 0)
         x_quant(1)
-        for i in (0, 1):
-            for t in range(NT):
-                mm1(t, i)
-            for t in range(NT):
-                d_centre(t, i)
+        quantise(uin_c[:, 256:512], uin_s[:, 256:512], uin_g[:, 256:512, :])
+        for t in (2, 3):
+            mm1(t, 0)
+        for t in (2, 3):
+            d_centre(t, 0)
+        for t in range(NT):
+            mm1(t, 1)
+        spread(taps, small, NSMALL, "tp")
+        for t in range(NT):
+            d_centre(t, 1)
         x_regroup(2, "G")
 
         d_pair(0, 1, 0)

@@ -43,9 +43,9 @@ def tile_lowrankconv3d_kernel(tc, x, U_kh, U_kw, U_kd, U_c_in, U_c_out, bias, ou
 
     with ExitStack() as ctx:
         keep = ctx.enter_context(tc.tile_pool(name="keep", bufs=1))
-        xgp = ctx.enter_context(tc.tile_pool(name="xgp", bufs=1))
+        xgp = ctx.enter_context(tc.tile_pool(name="xgp", bufs=2))
         upool = ctx.enter_context(tc.tile_pool(name="upool", bufs=8))
-        zpool = ctx.enter_context(tc.tile_pool(name="zpool", bufs=12))
+        zpool = ctx.enter_context(tc.tile_pool(name="zpool", bufs=10))
         ypool = ctx.enter_context(tc.tile_pool(name="ypool", bufs=3))
         opool = ctx.enter_context(tc.tile_pool(name="opool", bufs=12))
         ps = ctx.enter_context(tc.psum_pool(name="ps", bufs=8))
@@ -82,8 +82,7 @@ def tile_lowrankconv3d_kernel(tc, x, U_kh, U_kw, U_kd, U_c_in, U_c_out, bias, ou
         ys = {}
         po = {}
         ph = {}
-        p0 = {}
-        p2 = {}
+        pr = {}
 
         def tap(t, k):
             if k >= KD:
@@ -222,35 +221,30 @@ def tile_lowrankconv3d_kernel(tc, x, U_kh, U_kw, U_kd, U_c_in, U_c_out, bias, ou
                     op0=MULT, op1=ADD,
                 )
 
-        def h_scale(t, g):
+        def h_prod(t, g, k):
             lo, w = HG[g]
-            if lo >= SLICE:
-                p0[g] = zpool.tile([P, w], F32, name="p0_%d" % g, tag="p")
-                nc.scalar.activation(out=p0[g][:], in_=v[t][:, lo - SLICE : lo + w - SLICE], func=COPY, scale=tap(t, KH))
-            p2[g] = zpool.tile([P, w], F32, name="p2_%d" % g, tag="p")
-            nc.scalar.activation(out=p2[g][:], in_=v[t][:, lo + SLICE : lo + w + SLICE], func=COPY, scale=tap(t, KH + 2))
+            s = lo - SLICE if k == 0 else lo + SLICE
+            pr[(t, g, k)] = zpool.tile([P, w], F32, name="p%d_%d_%d" % (k, t, g), tag="p")
+            nc.scalar.activation(out=pr[(t, g, k)][:], in_=v[t][:, s : s + w], func=COPY, scale=tap(t, KH + k))
 
-        def h_centre_late(t, g, told):
-            lo, w = HG[g]
-            z[(t, g)] = z[(told, g)]
-            nc.scalar.activation(out=z[(t, g)][:], in_=v[t][:, lo : lo + w], func=COPY, scale=tap(t, KH + 1))
-
-        def h_add(t, g):
-            lo, w = HG[g]
+        def h_add(t, g, k):
+            need_y3(g)
             zz = z[(t, g)]
-            if lo >= SLICE:
-                nc.gpsimd.tensor_tensor(out=zz[:], in0=zz[:], in1=p0[g][:], op=ADD)
-            nc.gpsimd.tensor_tensor(out=y3[g][:, t, :], in0=zz[:], in1=p2[g][:], op=ADD)
+            dst = y3[g][:, t, :] if k == 2 else zz[:]
+            nc.gpsimd.tensor_tensor(out=dst, in0=zz[:], in1=pr[(t, g, k)][:], op=ADD)
 
         def h_triple(g):
             for k in (0, 2):
                 for t in TV:
                     h_side(t, g, k)
 
-        def y_regroup(g, eng):
+        def y_regroup(g, eng, a=0, b=None):
             w = HG[g][1]
-            y3g[g] = ypool.tile([P, w, PACK], BF16, name="y3g_%d" % g, tag="y3g", align_bytes=64)
-            regroup(eng, y3g[g][:], y3[g][:])
+            if b is None:
+                b = w
+            if g not in y3g:
+                y3g[g] = ypool.tile([P, w, PACK], BF16, name="y3g_%d" % g, tag="y3g", align_bytes=64)
+            regroup(eng, y3g[g][:, a:b, :], y3[g][:, :, a:b])
 
         def y_quant(g):
             w = HG[g][1]
@@ -327,6 +321,7 @@ def tile_lowrankconv3d_kernel(tc, x, U_kh, U_kw, U_kd, U_c_in, U_c_out, bias, ou
         for t in range(NT):
             d_centre(t, 1)
         x_regroup(2, "G")
+        x_regroup(3, "G", 0, 256)
 
         d_pair(0, 1, 0)
         d_pair(2, 3, 0)
@@ -338,6 +333,7 @@ def tile_lowrankconv3d_kernel(tc, x, U_kh, U_kw, U_kd, U_c_in, U_c_out, bias, ou
         d_pair(2, 3, 1)
         w_centre(2, 0)
         w_centre(3, 0)
+        regroup("S", uout_g[:, 0:256, :], uout_raw[:, :, 0:256])
         x_quant(2)
         for t in range(NT):
             mm1(t, 2)
@@ -347,29 +343,28 @@ def tile_lowrankconv3d_kernel(tc, x, U_kh, U_kw, U_kd, U_c_in, U_c_out, bias, ou
         d_centre(0, 2)
         d_centre(1, 2)
         w_pair(2, 3, 0)
+        h_prod(1, 0, 2)
+        h_add(1, 0, 2)
         h_centre(2, 0)
-        h_scale(3, 0)
         d_centre(2, 2)
+        h_prod(2, 0, 2)
+        h_add(2, 0, 2)
+        h_centre(3, 0)
+        h_prod(3, 0, 2)
+        h_add(3, 0, 2)
         d_centre(3, 2)
-        h_side(1, 0, 2)
-        h_side(2, 0, 2)
-        h_centre_late(3, 0, 1)
-        h_add(3, 0)
         ycopy(0)
-        x_regroup(3, "S", 0, 256)
         x_regroup(3, "S", 256, 512)
         y_regroup(0, "G")
 
         d_pair(0, 1, 2)
         w_centre(0, 1)
         w_centre(1, 1)
-        regroup("S", uout_g[:, 0:256, :], uout_raw[:, :, 0:256])
         d_pair(2, 3, 2)
         w_centre(2, 1)
         w_centre(3, 1)
         regroup("S", uout_g[:, 256:512, :], uout_raw[:, :, 256:512])
         x_quant(3)
-        y_quant(0)
         for t in range(NT):
             mm1(t, 3)
         w_pair(0, 1, 1)
@@ -377,20 +372,23 @@ def tile_lowrankconv3d_kernel(tc, x, U_kh, U_kw, U_kd, U_c_in, U_c_out, bias, ou
         h_centre(1, 1)
         d_centre(0, 3)
         d_centre(1, 3)
+        y_quant(0)
         w_pair(2, 3, 1)
         h_centre(2, 1)
-        h_scale(3, 1)
+        h_prod(3, 1, 0)
+        h_prod(3, 1, 2)
         quantise(uout_c[:], uout_s[:], uout_g[:])
         h_side(1, 1, 0)
         h_side(2, 1, 0)
         h_side(1, 1, 2)
         h_side(2, 1, 2)
         d_centre(2, 3)
-        h_centre_late(3, 1, 1)
-        h_add(3, 1)
         d_centre(3, 3)
+        h_centre(3, 1)
+        h_add(3, 1, 0)
+        h_add(3, 1, 2)
         ycopy(1)
-        x_regroup(4, "S", 0, 256)
+        x_regroup(4, "G", 0, 256)
         for o in range(NT):
             mm2(o, 0)
 
@@ -417,73 +415,82 @@ def tile_lowrankconv3d_kernel(tc, x, U_kh, U_kw, U_kd, U_c_in, U_c_out, bias, ou
         for o in range(3):
             mm2(o, 1)
         h_centre(2, 2)
-        h_centre(3, 2)
-        h_triple(2)
-        outp(0, 1, "S")
+        h_prod(3, 2, 0)
+        h_prod(3, 2, 2)
+        h_side(1, 2, 0)
+        h_side(2, 2, 0)
+        h_side(1, 2, 2)
+        h_side(2, 2, 2)
         mm2(3, 1)
         d_centre(0, 4)
         d_centre(1, 4)
+        h_centre(3, 2)
+        h_add(3, 2, 0)
+        h_add(3, 2, 2)
+        outp(0, 1, "S")
         ycopy(2)
         d_centre(2, 4)
         d_centre(3, 4)
         outp(1, 1, "S")
-        y_regroup(2, "G")
 
         d_pair(0, 1, 4)
-        outp(2, 1, "S")
         w_centre(0, 3)
         w_centre(1, 3)
-        outp(3, 1, "S")
+        y_regroup(2, "G", 0, 256)
+        y_regroup(2, "S", 256, 512)
         d_pair(2, 3, 4)
         w_centre(2, 3)
         w_centre(3, 3)
+        outp(2, 1, "S")
+        outp(3, 1, "S")
+        w_pair(0, 1, 3)
         y_quant(2)
         for o in range(NT):
             mm2(o, 2)
-        w_pair(0, 1, 3)
         h_pe(3)
         h_pe(4)
-        h_pe(5)
         h_centre(1, 3)
         h_centre(1, 4)
         outp(0, 2, "S")
-        outp(1, 2, "S")
         h_centre(1, 5)
         w_pair(2, 3, 3)
+        outp(1, 2, "S")
         h_centre(2, 3)
         h_centre(3, 3)
         ycopy(3)
-        h_centre(2, 4)
-        h_centre(3, 4)
-        ycopy(4)
+        outp(2, 2, "S")
         for t in TV:
             h_side(t, 3, 0)
-        y_regroup(3, "S")
-        h_centre(2, 5)
-        h_centre(3, 5)
-        ycopy(5)
-        h_triple(4)
-        y_regroup(4, "V")
+        y_regroup(3, "V")
+        h_centre(2, 4)
+        h_centre(3, 4)
+        outp(3, 2, "S")
         y_quant(3)
         for o in range(NT):
             mm2(o, 3)
-        outp(2, 2, "S")
-        outp(3, 2, "S")
-        for t in TV:
-            h_side(t, 5, 0)
+        h_pe(5)
+        ycopy(4)
+        h_centre(2, 5)
+        h_centre(3, 5)
+        h_triple(4)
+        outp(0, 3, "S")
+        outp(1, 3, "S")
+        y_regroup(4, "S")
+        for k in (0, 2):
+            for t in TV:
+                h_side(t, 5, k)
+        ycopy(5)
+        outp(2, 3, "S")
+        outp(3, 3, "S")
         y_quant(4)
         for o in range(NT):
             mm2(o, 4)
-        for o in range(NT):
-            outp(o, 3, "S")
-        for t in TV:
-            h_side(t, 5, 2)
         y_regroup(5, "V")
-        outp(0, 4, "V")
+        outp(0, 4, "S")
+        outp(1, 4, "S")
         y_quant(5)
         for o in range(NT):
             mm2(o, 5)
-        outp(1, 4, "S")
         outp(2, 4, "V")
         outp(3, 4, "S")
         outp(0, 5, "V")

@@ -43,7 +43,7 @@ def tile_lowrankconv3d_kernel(tc, x, U_kh, U_kw, U_kd, U_c_in, U_c_out, bias, ou
 
     with ExitStack() as ctx:
         keep = ctx.enter_context(tc.tile_pool(name="keep", bufs=1))
-        xgp = ctx.enter_context(tc.tile_pool(name="xgp", bufs=2))
+        xgp = ctx.enter_context(tc.tile_pool(name="xgp", bufs=1))
         upool = ctx.enter_context(tc.tile_pool(name="upool", bufs=8))
         zpool = ctx.enter_context(tc.tile_pool(name="zpool", bufs=10))
         ypool = ctx.enter_context(tc.tile_pool(name="ypool", bufs=3))
@@ -57,7 +57,7 @@ def tile_lowrankconv3d_kernel(tc, x, U_kh, U_kw, U_kd, U_c_in, U_c_out, bias, ou
         warm2 = keep.tile([P, 8], F32, name="warm2")
         ident = keep.tile([P, P], BF16, name="ident")
         ident32 = keep.tile([P, P], F32, name="ident32")
-        diag = [keep.tile([P, P], F32, name="diag%d" % k) for k in range(3)]
+        diag = {}
         tapsd = keep.tile([P, NT, 3], F32, name="tapsd")
         taps = keep.tile([P, NT, NSMALL], F32, name="taps")
         uin_raw = keep.tile([P, PACK, 512], BF16, name="uin_raw")
@@ -112,39 +112,41 @@ def tile_lowrankconv3d_kernel(tc, x, U_kh, U_kw, U_kd, U_c_in, U_c_out, bias, ou
             if b is None:
                 b = w
             if i not in xg:
-                xg[i] = xgp.tile([P, w, PACK], BF16, name="xg%d" % i, tag="xg", align_bytes=64)
+                xg[i] = xgp.tile([P, w, PACK], BF16, name="xg%d" % i, tag="xgodd" if i == 3 else "xg", align_bytes=64)
             regroup(eng, xg[i][:, a:b, :], xraw[i][:, :, a:b])
 
         def x_quant(i):
             quantise(xc[i][:], xs[i][:], xg[i][:])
 
-        def mm1(t, i):
-            w = XP[i][1]
-            y0[(t, i)] = ps.tile([P, w], F32, name="y0_%d_%d" % (t, i), tag="ps")
-            nc.tensor.matmul_mx(
-                out=y0[(t, i)][:],
-                lhsT=uin_c[:, t * P : (t + 1) * P].bitcast(FP8X4),
-                lhsT_scale=uin_s[:, t * P : (t + 1) * P],
-                rhs=xc[i][:].bitcast(FP8X4),
-                rhs_scale=xs[i][:],
-                start=True,
-                stop=True,
-            )
+        def mm1(t, *pieces):
+            lo = XP[pieces[0]][0]
+            w = sum(XP[i][1] for i in pieces)
+            y0[(t, lo)] = ps.tile([P, w], F32, name="y0_%d_%d" % (t, lo), tag="ps")
+            for i in pieces:
+                o = XP[i][0] - lo
+                nc.tensor.matmul_mx(
+                    out=y0[(t, lo)][:, o : o + XP[i][1]],
+                    lhsT=uin_c[:, t * P : (t + 1) * P].bitcast(FP8X4),
+                    lhsT_scale=uin_s[:, t * P : (t + 1) * P],
+                    rhs=xc[i][:].bitcast(FP8X4),
+                    rhs_scale=xs[i][:],
+                    start=True,
+                    stop=True,
+                )
 
-        def d_centre(t, i):
-            lo, w = XP[i]
+        def u_part(t, lo):
             c = lo // CHUNK
-            o = lo % CHUNK
             if (t, c) not in u:
                 u[(t, c)] = upool.tile([P, CHUNK], F32, name="u_%d_%d" % (t, c), tag="u")
-            nc.scalar.activation(out=u[(t, c)][:, o : o + w], in_=y0[(t, i)][:], func=COPY, scale=tap(t, KD + 1))
-
-        def d_side(t, i, k):
-            lo, w = XP[i]
-            c = lo // CHUNK
             o = lo % CHUNK
-            uu = u[(t, c)][:, o : o + w].rearrange("p (r d) -> p r d", d=ROW)
-            yy = y0[(t, i)][:].rearrange("p (r d) -> p r d", d=ROW)
+            return u[(t, c)][:, o : o + y0[(t, lo)].shape[1]]
+
+        def d_centre(t, lo):
+            nc.scalar.activation(out=u_part(t, lo), in_=y0[(t, lo)][:], func=COPY, scale=tap(t, KD + 1))
+
+        def d_side(t, lo, k):
+            uu = u_part(t, lo).rearrange("p (r d) -> p r d", d=ROW)
+            yy = y0[(t, lo)][:].rearrange("p (r d) -> p r d", d=ROW)
             if k == 0:
                 dst, src = uu[:, :, 1:ROW], yy[:, :, 0 : ROW - 1]
             else:
@@ -196,8 +198,28 @@ def tile_lowrankconv3d_kernel(tc, x, U_kh, U_kw, U_kd, U_c_in, U_c_out, bias, ou
                 terms.append((2, lo + SLICE))
             for n, (k, s) in enumerate(terms):
                 nc.tensor.matmul(
-                    out=ph[g][:], lhsT=diag[k][:], rhs=v[TPE][:, s : s + w], start=(n == 0), stop=(n == len(terms) - 1)
+                    out=ph[g][:], lhsT=diag[(TPE, k)][:], rhs=v[TPE][:, s : s + w], start=(n == 0), stop=(n == len(terms) - 1)
                 )
+
+        def make_diag(t, k):
+            diag[(t, k)] = keep.tile([P, P], F32, name="diag%d_%d" % (t, k))
+            nc.scalar.activation(out=diag[(t, k)][:], in_=ident32[:], func=COPY, scale=tap(t, KH + k))
+
+        def h_pe2(t, g):
+            lo, w = HG[g]
+            ph[(t, g)] = ps.tile([P, w], F32, name="ph_%d_%d" % (t, g), tag="ps")
+            for k, s in ((1, lo), (0, lo - SLICE)):
+                nc.tensor.matmul(
+                    out=ph[(t, g)][:], lhsT=diag[(t, k)][:], rhs=v[t][:, s : s + w], start=(k == 1), stop=(k == 0)
+                )
+
+        def h_last(t, g):
+            lo, w = HG[g]
+            need_y3(g)
+            nc.vector.scalar_tensor_tensor(
+                out=y3[g][:, t, :], in0=v[t][:, lo + SLICE : lo + w + SLICE], scalar=tap(t, KH + 2), in1=ph[(t, g)][:],
+                op0=MULT, op1=ADD,
+            )
 
         def ycopy(g):
             need_y3(g)
@@ -288,7 +310,8 @@ def tile_lowrankconv3d_kernel(tc, x, U_kh, U_kw, U_kd, U_c_in, U_c_out, bias, ou
         nc.sync.dma_start(out=small[KW : KW + 3, :], in_=U_kw)
         nc.sync.dma_start(out=small[KH : KH + 3, :], in_=U_kh)
         nc.sync.dma_start(out=small[KB : KB + 1, :], in_=bias.rearrange("(a n) -> a n", a=1))
-        for i in range(2, len(XP)):
+        nc.sync.dma_start(out=xraw[2][:], in_=xv[:, :, XP[2][0] : XP[2][0] + XP[2][1]])
+        for i in range(3, len(XP)):
             nc.sync.dma_start(out=xraw[i][:], in_=xv[:, :, XP[i][0] : XP[i][0] + XP[i][1]])
         nc.sync.dma_start(out=uout_raw[:], in_=uoutv)
 
@@ -309,58 +332,53 @@ def tile_lowrankconv3d_kernel(tc, x, U_kh, U_kw, U_kd, U_c_in, U_c_out, bias, ou
             mm1(t, 0)
         for t in (0, 1):
             d_centre(t, 0)
-        x_quant(1)
         quantise(uin_c[:, 256:512], uin_s[:, 256:512], uin_g[:, 256:512, :])
+        x_quant(1)
+        for t in (0, 1):
+            mm1(t, 1)
+        for t in (0, 1):
+            d_centre(t, 256)
         for t in (2, 3):
-            mm1(t, 0)
+            mm1(t, 0, 1)
         for t in (2, 3):
             d_centre(t, 0)
-        for t in range(NT):
-            mm1(t, 1)
         spread(taps, small, NSMALL, "tp")
-        for t in range(NT):
-            d_centre(t, 1)
         x_regroup(2, "G")
         x_regroup(3, "G", 0, 256)
 
         d_pair(0, 1, 0)
-        d_pair(2, 3, 0)
-        for k in range(3):
-            nc.scalar.activation(out=diag[k][:], in_=ident32[:], func=COPY, scale=tap(TPE, KH + k))
-        d_pair(0, 1, 1)
+        d_pair(0, 1, 256)
         w_centre(0, 0)
         w_centre(1, 0)
-        d_pair(2, 3, 1)
+        d_pair(2, 3, 0)
         w_centre(2, 0)
         w_centre(3, 0)
         regroup("S", uout_g[:, 0:256, :], uout_raw[:, :, 0:256])
+        for t, k in ((0, 1), (0, 0), (1, 1), (1, 0), (0, 2)):
+            make_diag(t, k)
         x_quant(2)
         for t in range(NT):
             mm1(t, 2)
         w_pair(0, 1, 0)
-        h_pe(0)
+        h_centre(0, 0)
         h_centre(1, 0)
-        d_centre(0, 2)
-        d_centre(1, 2)
         w_pair(2, 3, 0)
+        for t in range(NT):
+            d_centre(t, 512)
+        h_prod(0, 0, 2)
+        h_add(0, 0, 2)
         h_prod(1, 0, 2)
         h_add(1, 0, 2)
-        h_centre(2, 0)
-        d_centre(2, 2)
-        h_prod(2, 0, 2)
-        h_add(2, 0, 2)
-        h_centre(3, 0)
-        h_prod(3, 0, 2)
-        h_add(3, 0, 2)
-        d_centre(3, 2)
-        ycopy(0)
+        for t in (2, 3):
+            h_centre(t, 0)
+            h_prod(t, 0, 2)
+            h_add(t, 0, 2)
         x_regroup(3, "S", 256, 512)
-        y_regroup(0, "G")
 
-        d_pair(0, 1, 2)
+        d_pair(0, 1, 512)
         w_centre(0, 1)
         w_centre(1, 1)
-        d_pair(2, 3, 2)
+        d_pair(2, 3, 512)
         w_centre(2, 1)
         w_centre(3, 1)
         regroup("S", uout_g[:, 256:512, :], uout_raw[:, :, 256:512])
@@ -368,36 +386,37 @@ def tile_lowrankconv3d_kernel(tc, x, U_kh, U_kw, U_kd, U_c_in, U_c_out, bias, ou
         for t in range(NT):
             mm1(t, 3)
         w_pair(0, 1, 1)
-        h_pe(1)
-        h_centre(1, 1)
-        d_centre(0, 3)
-        d_centre(1, 3)
-        y_quant(0)
+        h_pe2(0, 1)
+        h_pe2(1, 1)
+        d_centre(0, 1024)
+        d_centre(1, 1024)
+        y_regroup(0, "S")
         w_pair(2, 3, 1)
+        y_quant(0)
         h_centre(2, 1)
         h_prod(3, 1, 0)
         h_prod(3, 1, 2)
+        h_prod(2, 1, 2)
         quantise(uout_c[:], uout_s[:], uout_g[:])
-        h_side(1, 1, 0)
         h_side(2, 1, 0)
-        h_side(1, 1, 2)
-        h_side(2, 1, 2)
-        d_centre(2, 3)
-        d_centre(3, 3)
+        h_last(0, 1)
         h_centre(3, 1)
+        d_centre(2, 1024)
+        d_centre(3, 1024)
         h_add(3, 1, 0)
         h_add(3, 1, 2)
-        ycopy(1)
-        x_regroup(4, "G", 0, 256)
+        h_add(2, 1, 2)
+        x_regroup(4, "S", 0, 256)
         for o in range(NT):
             mm2(o, 0)
 
-        d_pair(0, 1, 3)
+        d_pair(0, 1, 1024)
+        h_last(1, 1)
         w_centre(0, 2)
         w_centre(1, 2)
         x_regroup(4, "S", 256, 512)
         outp(0, 0, "S")
-        d_pair(2, 3, 3)
+        d_pair(2, 3, 1024)
         w_centre(2, 2)
         w_centre(3, 2)
         outp(1, 0, "S")
@@ -408,8 +427,8 @@ def tile_lowrankconv3d_kernel(tc, x, U_kh, U_kw, U_kd, U_c_in, U_c_out, bias, ou
         for t in range(NT):
             mm1(t, 4)
         w_pair(0, 1, 2)
-        h_pe(2)
-        h_centre(1, 2)
+        h_pe2(0, 2)
+        h_pe2(1, 2)
         w_pair(2, 3, 2)
         y_quant(1)
         for o in range(3):
@@ -417,28 +436,27 @@ def tile_lowrankconv3d_kernel(tc, x, U_kh, U_kw, U_kd, U_c_in, U_c_out, bias, ou
         h_centre(2, 2)
         h_prod(3, 2, 0)
         h_prod(3, 2, 2)
-        h_side(1, 2, 0)
         h_side(2, 2, 0)
-        h_side(1, 2, 2)
+        h_last(0, 2)
         h_side(2, 2, 2)
         mm2(3, 1)
-        d_centre(0, 4)
-        d_centre(1, 4)
+        d_centre(0, 1536)
+        d_centre(1, 1536)
         h_centre(3, 2)
         h_add(3, 2, 0)
         h_add(3, 2, 2)
         outp(0, 1, "S")
-        ycopy(2)
-        d_centre(2, 4)
-        d_centre(3, 4)
+        d_centre(2, 1536)
+        d_centre(3, 1536)
         outp(1, 1, "S")
 
-        d_pair(0, 1, 4)
+        d_pair(0, 1, 1536)
+        h_last(1, 2)
         w_centre(0, 3)
         w_centre(1, 3)
         y_regroup(2, "G", 0, 256)
         y_regroup(2, "S", 256, 512)
-        d_pair(2, 3, 4)
+        d_pair(2, 3, 1536)
         w_centre(2, 3)
         w_centre(3, 3)
         outp(2, 1, "S")
@@ -457,14 +475,17 @@ def tile_lowrankconv3d_kernel(tc, x, U_kh, U_kw, U_kd, U_c_in, U_c_out, bias, ou
         outp(1, 2, "S")
         h_centre(2, 3)
         h_centre(3, 3)
-        ycopy(3)
         outp(2, 2, "S")
-        for t in TV:
-            h_side(t, 3, 0)
-        y_regroup(3, "V")
         h_centre(2, 4)
         h_centre(3, 4)
+        ycopy(3)
         outp(3, 2, "S")
+        for t in TV:
+            h_side(t, 3, 0)
+        for t in TV:
+            h_side(t, 4, 0)
+        y_regroup(3, "V")
+        h_side(1, 4, 2)
         y_quant(3)
         for o in range(NT):
             mm2(o, 3)
@@ -472,7 +493,8 @@ def tile_lowrankconv3d_kernel(tc, x, U_kh, U_kw, U_kd, U_c_in, U_c_out, bias, ou
         ycopy(4)
         h_centre(2, 5)
         h_centre(3, 5)
-        h_triple(4)
+        h_side(2, 4, 2)
+        h_side(3, 4, 2)
         outp(0, 3, "S")
         outp(1, 3, "S")
         y_regroup(4, "S")

@@ -188,30 +188,20 @@ def tile_lowrankconv3d_kernel(tc, x, U_kh, U_kw, U_kd, U_c_in, U_c_out, bias, ou
             if g not in y3:
                 y3[g] = ypool.tile([P, NT, HG[g][1]], BF16, name="y3_%d" % g, tag="y3")
 
-        def h_pe(g):
+        def h_pe(t, g, ks, start=False, stop=False):
             lo, w = HG[g]
-            ph[g] = ps.tile([P, w], F32, name="ph_%d" % g, tag="ps")
-            terms = [(1, lo)]
-            if lo >= SLICE:
-                terms.append((0, lo - SLICE))
-            if lo + w < NPOS:
-                terms.append((2, lo + SLICE))
-            for n, (k, s) in enumerate(terms):
+            if start:
+                ph[(t, g)] = ps.tile([P, w], F32, name="ph_%d_%d" % (t, g), tag="ps")
+            for n, k in enumerate(ks):
+                s = lo + (k - 1) * SLICE
                 nc.tensor.matmul(
-                    out=ph[g][:], lhsT=diag[(TPE, k)][:], rhs=v[TPE][:, s : s + w], start=(n == 0), stop=(n == len(terms) - 1)
+                    out=ph[(t, g)][:], lhsT=diag[(t, k)][:], rhs=v[t][:, s : s + w],
+                    start=start and n == 0, stop=stop and n == len(ks) - 1,
                 )
 
         def make_diag(t, k):
             diag[(t, k)] = keep.tile([P, P], F32, name="diag%d_%d" % (t, k))
             nc.scalar.activation(out=diag[(t, k)][:], in_=ident32[:], func=COPY, scale=tap(t, KH + k))
-
-        def h_pe2(t, g):
-            lo, w = HG[g]
-            ph[(t, g)] = ps.tile([P, w], F32, name="ph_%d_%d" % (t, g), tag="ps")
-            for k, s in ((1, lo), (0, lo - SLICE)):
-                nc.tensor.matmul(
-                    out=ph[(t, g)][:], lhsT=diag[(t, k)][:], rhs=v[t][:, s : s + w], start=(k == 1), stop=(k == 0)
-                )
 
         def h_last(t, g):
             lo, w = HG[g]
@@ -223,7 +213,7 @@ def tile_lowrankconv3d_kernel(tc, x, U_kh, U_kw, U_kd, U_c_in, U_c_out, bias, ou
 
         def ycopy(g):
             need_y3(g)
-            nc.scalar.copy(out=y3[g][:, TPE, :], in_=ph[g][:])
+            nc.scalar.copy(out=y3[g][:, TPE, :], in_=ph[(TPE, g)][:])
 
         def h_side(t, g, k):
             lo, w = HG[g]
@@ -322,8 +312,8 @@ def tile_lowrankconv3d_kernel(tc, x, U_kh, U_kw, U_kd, U_c_in, U_c_out, bias, ou
             nc.scalar.copy(out=dst[:], in_=tp[:, :, 0:n])
 
         x_regroup(0, "V")
-        x_quant(0)
         regroup("V", uin_g[:, 0:256, :], uin_raw[:, :, 0:256])
+        x_quant(0)
         spread(tapsd, smalld, 3, "tpd")
         regroup("S", uin_g[:, 256:512, :], uin_raw[:, :, 256:512])
         quantise(uin_c[:, 0:256], uin_s[:, 0:256], uin_g[:, 0:256, :])
@@ -386,8 +376,8 @@ def tile_lowrankconv3d_kernel(tc, x, U_kh, U_kw, U_kd, U_c_in, U_c_out, bias, ou
         for t in range(NT):
             mm1(t, 3)
         w_pair(0, 1, 1)
-        h_pe2(0, 1)
-        h_pe2(1, 1)
+        for t in (0, 1):
+            h_pe(t, 1, (1, 0), start=True, stop=True)
         d_centre(0, 1024)
         d_centre(1, 1024)
         y_regroup(0, "S")
@@ -427,8 +417,8 @@ def tile_lowrankconv3d_kernel(tc, x, U_kh, U_kw, U_kd, U_c_in, U_c_out, bias, ou
         for t in range(NT):
             mm1(t, 4)
         w_pair(0, 1, 2)
-        h_pe2(0, 2)
-        h_pe2(1, 2)
+        for t in (0, 1):
+            h_pe(t, 2, (1, 0), start=True, stop=True)
         w_pair(2, 3, 2)
         y_quant(1)
         for o in range(3):
@@ -445,9 +435,9 @@ def tile_lowrankconv3d_kernel(tc, x, U_kh, U_kw, U_kd, U_c_in, U_c_out, bias, ou
         h_centre(3, 2)
         h_add(3, 2, 0)
         h_add(3, 2, 2)
-        outp(0, 1, "S")
         d_centre(2, 1536)
         d_centre(3, 1536)
+        outp(0, 1, "S")
         outp(1, 1, "S")
 
         d_pair(0, 1, 1536)
@@ -456,6 +446,8 @@ def tile_lowrankconv3d_kernel(tc, x, U_kh, U_kw, U_kd, U_c_in, U_c_out, bias, ou
         w_centre(1, 3)
         y_regroup(2, "G", 0, 256)
         y_regroup(2, "S", 256, 512)
+        h_pe(TPE, 4, (1, 0), start=True)
+        h_pe(TPE, 5, (0,), start=True)
         d_pair(2, 3, 1536)
         w_centre(2, 3)
         w_centre(3, 3)
@@ -465,8 +457,8 @@ def tile_lowrankconv3d_kernel(tc, x, U_kh, U_kw, U_kd, U_c_in, U_c_out, bias, ou
         y_quant(2)
         for o in range(NT):
             mm2(o, 2)
-        h_pe(3)
-        h_pe(4)
+        h_pe(TPE, 3, (0, 1), start=True, stop=True)
+        h_pe(TPE, 4, (2,), stop=True)
         h_centre(1, 3)
         h_centre(1, 4)
         outp(0, 2, "S")
@@ -480,27 +472,29 @@ def tile_lowrankconv3d_kernel(tc, x, U_kh, U_kw, U_kd, U_c_in, U_c_out, bias, ou
         h_centre(3, 4)
         ycopy(3)
         outp(3, 2, "S")
-        for t in TV:
-            h_side(t, 3, 0)
-        for t in TV:
-            h_side(t, 4, 0)
+        for g in (3, 4, 5):
+            h_side(1, g, 0)
+        for g in (3, 4):
+            h_side(2, g, 0)
+            h_side(3, g, 0)
         y_regroup(3, "V")
         h_side(1, 4, 2)
         y_quant(3)
         for o in range(NT):
             mm2(o, 3)
-        h_pe(5)
-        ycopy(4)
+        h_pe(TPE, 5, (1, 2), stop=True)
         h_centre(2, 5)
         h_centre(3, 5)
+        ycopy(4)
         h_side(2, 4, 2)
         h_side(3, 4, 2)
         outp(0, 3, "S")
         outp(1, 3, "S")
         y_regroup(4, "S")
-        for k in (0, 2):
-            for t in TV:
-                h_side(t, 5, k)
+        h_side(2, 5, 0)
+        h_side(3, 5, 0)
+        for t in TV:
+            h_side(t, 5, 2)
         ycopy(5)
         outp(2, 3, "S")
         outp(3, 3, "S")

@@ -31,6 +31,7 @@ TV = (1, 2, 3)
 FLOPS = 2 * 2 * 512 * 512 * NPOS + 2 * 9 * 512 * NPOS
 
 XP = ((0, 256), (256, 256), (512, 512), (1024, 512), (1536, 512))
+GJOIN = (0, 1, 2)
 HG = ((0, 256), (256, 512), (768, 512), (1792, 256), (1280, 256), (1536, 256))
 
 
@@ -46,6 +47,7 @@ def tile_lowrankconv3d_kernel(tc, x, U_kh, U_kw, U_kd, U_c_in, U_c_out, bias, ou
         xgp = ctx.enter_context(tc.tile_pool(name="xgp", bufs=1))
         upool = ctx.enter_context(tc.tile_pool(name="upool", bufs=8))
         zpool = ctx.enter_context(tc.tile_pool(name="zpool", bufs=10))
+        zrpool = ctx.enter_context(tc.tile_pool(name="zrpool", bufs=1))
         ypool = ctx.enter_context(tc.tile_pool(name="ypool", bufs=3))
         opool = ctx.enter_context(tc.tile_pool(name="opool", bufs=12))
         ps = ctx.enter_context(tc.psum_pool(name="ps", bufs=8))
@@ -83,6 +85,7 @@ def tile_lowrankconv3d_kernel(tc, x, U_kh, U_kw, U_kd, U_c_in, U_c_out, bias, ou
         po = {}
         ph = {}
         pr = {}
+        zr = {}
 
         def tap(t, k):
             if k >= KD:
@@ -179,10 +182,41 @@ def tile_lowrankconv3d_kernel(tc, x, U_kh, U_kw, U_kd, U_c_in, U_c_out, bias, ou
             w_side(a, c, 2)
             w_side(b, c, 2)
 
+        def need_zr(g):
+            if g not in zr:
+                w = HG[g][1]
+                zr[g] = (
+                    zrpool.tile([P, NT, w], F32, name="zz_%d" % g, tag="zz"),
+                    zrpool.tile([P, NT, w], F32, name="rr_%d" % g, tag="rr"),
+                )
+
         def h_centre(t, g):
             lo, w = HG[g]
-            z[(t, g)] = zpool.tile([P, w], F32, name="z_%d_%d" % (t, g), tag="z")
-            nc.scalar.activation(out=z[(t, g)][:], in_=v[t][:, lo : lo + w], func=COPY, scale=tap(t, KH + 1))
+            if g in GJOIN:
+                need_zr(g)
+                z[(t, g)] = zr[g][0][:, t, :]
+            else:
+                z[(t, g)] = zpool.tile([P, w], F32, name="z_%d_%d" % (t, g), tag="z")
+            nc.scalar.activation(out=z[(t, g)][:, 0:w], in_=v[t][:, lo : lo + w], func=COPY, scale=tap(t, KH + 1))
+
+        def h_last_prod(t, g, a=0, b=None):
+            lo, w = HG[g]
+            if b is None:
+                b = w
+            need_zr(g)
+            s = lo + SLICE
+            nc.scalar.activation(out=zr[g][1][:, t, a:b], in_=v[t][:, s + a : s + b], func=COPY, scale=tap(t, KH + 2))
+
+        def h_join(g, a, b):
+            w = HG[g][1]
+            if g not in y3g:
+                y3g[g] = ypool.tile([P, w, PACK], BF16, name="y3g_%d" % g, tag="y3g", align_bytes=64)
+            nc.gpsimd.tensor_tensor(
+                out=y3g[g][:, a:b, :].rearrange("p (c i) t -> p c t i", i=4),
+                in0=zr[g][0][:, :, a:b].rearrange("p t (c i) -> p c t i", i=4),
+                in1=zr[g][1][:, :, a:b].rearrange("p t (c i) -> p c t i", i=4),
+                op=ADD,
+            )
 
         def need_y3(g):
             if g not in y3:
@@ -198,6 +232,19 @@ def tile_lowrankconv3d_kernel(tc, x, U_kh, U_kw, U_kd, U_c_in, U_c_out, bias, ou
                     out=ph[(t, g)][:], lhsT=diag[(t, k)][:], rhs=v[t][:, s : s + w],
                     start=start and n == 0, stop=stop and n == len(ks) - 1,
                 )
+
+        def h_pe_part(t, g, a, b):
+            lo = HG[g][0]
+            ph[(t, g, a)] = ps.tile([P, b - a], F32, name="ph_%d_%d_%d" % (t, g, a), tag="ps")
+            for k in (1, 0):
+                s = lo + (k - 1) * SLICE
+                nc.tensor.matmul(
+                    out=ph[(t, g, a)][:], lhsT=diag[(t, k)][:], rhs=v[t][:, s + a : s + b], start=k == 1, stop=k == 0
+                )
+
+        def z_copy(t, g, a, b):
+            need_zr(g)
+            nc.scalar.copy(out=zr[g][0][:, t, a:b], in_=ph[(t, g, a)][:])
 
         def make_diag(t, k):
             diag[(t, k)] = keep.tile([P, P], F32, name="diag%d_%d" % (t, k))
@@ -218,7 +265,7 @@ def tile_lowrankconv3d_kernel(tc, x, U_kh, U_kw, U_kd, U_c_in, U_c_out, bias, ou
         def h_side(t, g, k):
             lo, w = HG[g]
             need_y3(g)
-            zz = z[(t, g)]
+            zz = z[(t, g)][:, 0:w]
             last = lo + w == NPOS
             if k == 0:
                 a = max(lo, SLICE)
@@ -312,8 +359,8 @@ def tile_lowrankconv3d_kernel(tc, x, U_kh, U_kw, U_kd, U_c_in, U_c_out, bias, ou
             nc.scalar.copy(out=dst[:], in_=tp[:, :, 0:n])
 
         x_regroup(0, "V")
-        regroup("V", uin_g[:, 0:256, :], uin_raw[:, :, 0:256])
         x_quant(0)
+        regroup("V", uin_g[:, 0:256, :], uin_raw[:, :, 0:256])
         spread(tapsd, smalld, 3, "tpd")
         regroup("S", uin_g[:, 256:512, :], uin_raw[:, :, 256:512])
         quantise(uin_c[:, 0:256], uin_s[:, 0:256], uin_g[:, 0:256, :])
@@ -353,16 +400,17 @@ def tile_lowrankconv3d_kernel(tc, x, U_kh, U_kw, U_kd, U_c_in, U_c_out, bias, ou
         h_centre(0, 0)
         h_centre(1, 0)
         w_pair(2, 3, 0)
-        for t in range(NT):
-            d_centre(t, 512)
-        h_prod(0, 0, 2)
-        h_add(0, 0, 2)
-        h_prod(1, 0, 2)
-        h_add(1, 0, 2)
+        d_centre(0, 512)
+        d_centre(1, 512)
+        h_last_prod(0, 0)
+        h_last_prod(1, 0)
         for t in (2, 3):
             h_centre(t, 0)
-            h_prod(t, 0, 2)
-            h_add(t, 0, 2)
+            h_last_prod(t, 0)
+        h_join(0, 0, 256)
+        d_centre(2, 512)
+        d_centre(3, 512)
+        x_regroup(4, "G", 0, 256)
         x_regroup(3, "S", 256, 512)
 
         d_pair(0, 1, 512)
@@ -376,76 +424,84 @@ def tile_lowrankconv3d_kernel(tc, x, U_kh, U_kw, U_kd, U_c_in, U_c_out, bias, ou
         for t in range(NT):
             mm1(t, 3)
         w_pair(0, 1, 1)
-        for t in (0, 1):
-            h_pe(t, 1, (1, 0), start=True, stop=True)
+        for a in (0, 256):
+            for t in (0, 1):
+                h_pe_part(t, 1, a, a + 256)
         d_centre(0, 1024)
         d_centre(1, 1024)
-        y_regroup(0, "S")
+        h_last_prod(0, 1)
+        h_last_prod(1, 1)
         w_pair(2, 3, 1)
         y_quant(0)
         h_centre(2, 1)
-        h_prod(3, 1, 0)
-        h_prod(3, 1, 2)
-        h_prod(2, 1, 2)
+        h_centre(3, 1)
         quantise(uout_c[:], uout_s[:], uout_g[:])
         h_side(2, 1, 0)
-        h_last(0, 1)
-        h_centre(3, 1)
+        h_side(3, 1, 0)
+        for t in (2, 3):
+            h_last_prod(t, 1, 0, 256)
+        for t in (0, 1):
+            z_copy(t, 1, 0, 256)
+        h_join(1, 0, 256)
         d_centre(2, 1024)
         d_centre(3, 1024)
-        h_add(3, 1, 0)
-        h_add(3, 1, 2)
-        h_add(2, 1, 2)
-        x_regroup(4, "S", 0, 256)
+        for t in (2, 3):
+            h_last_prod(t, 1, 256, 512)
+        for t in (0, 1):
+            z_copy(t, 1, 256, 512)
+        h_join(1, 256, 512)
         for o in range(NT):
             mm2(o, 0)
 
         d_pair(0, 1, 1024)
-        h_last(1, 1)
+        x_regroup(4, "S", 256, 512)
         w_centre(0, 2)
         w_centre(1, 2)
-        x_regroup(4, "S", 256, 512)
         outp(0, 0, "S")
         d_pair(2, 3, 1024)
         w_centre(2, 2)
         w_centre(3, 2)
         outp(1, 0, "S")
-        y_regroup(1, "S")
         outp(2, 0, "S")
         outp(3, 0, "S")
         x_quant(4)
         for t in range(NT):
             mm1(t, 4)
         w_pair(0, 1, 2)
-        for t in (0, 1):
-            h_pe(t, 2, (1, 0), start=True, stop=True)
+        for a in (0, 256):
+            for t in (0, 1):
+                h_pe_part(t, 2, a, a + 256)
+        d_centre(0, 1536)
+        d_centre(1, 1536)
+        h_last_prod(0, 2)
+        h_last_prod(1, 2)
         w_pair(2, 3, 2)
         y_quant(1)
         for o in range(3):
             mm2(o, 1)
         h_centre(2, 2)
-        h_prod(3, 2, 0)
-        h_prod(3, 2, 2)
-        h_side(2, 2, 0)
-        h_last(0, 2)
-        h_side(2, 2, 2)
-        mm2(3, 1)
-        d_centre(0, 1536)
-        d_centre(1, 1536)
         h_centre(3, 2)
-        h_add(3, 2, 0)
-        h_add(3, 2, 2)
+        h_side(2, 2, 0)
+        h_side(3, 2, 0)
+        for t in (2, 3):
+            h_last_prod(t, 2, 0, 256)
+        for t in (0, 1):
+            z_copy(t, 2, 0, 256)
+        h_join(2, 0, 256)
         d_centre(2, 1536)
         d_centre(3, 1536)
+        for t in (2, 3):
+            h_last_prod(t, 2, 256, 512)
+        for t in (0, 1):
+            z_copy(t, 2, 256, 512)
+        h_join(2, 256, 512)
+        mm2(3, 1)
         outp(0, 1, "S")
         outp(1, 1, "S")
 
         d_pair(0, 1, 1536)
-        h_last(1, 2)
         w_centre(0, 3)
         w_centre(1, 3)
-        y_regroup(2, "G", 0, 256)
-        y_regroup(2, "S", 256, 512)
         h_pe(TPE, 4, (1, 0), start=True)
         h_pe(TPE, 5, (0,), start=True)
         d_pair(2, 3, 1536)

@@ -199,6 +199,14 @@ def tile_lowrankconv3d_kernel(tc, x, U_kh, U_kw, U_kd, U_c_in, U_c_out, bias, ou
                 z[(t, g)] = zpool.tile([P, w], F32, name="z_%d_%d" % (t, g), tag="z")
             nc.scalar.activation(out=z[(t, g)][:, 0:w], in_=v[t][:, lo : lo + w], func=COPY, scale=tap(t, KH + 1))
 
+        def h_centre_g(t, g):
+            lo, w = HG[g]
+            need_zr(g)
+            z[(t, g)] = zr[g][0][:, t, :]
+            nc.gpsimd.tensor_scalar(
+                out=z[(t, g)], in0=v[t][:, lo : lo + w], scalar1=tap(t, KH + 1), scalar2=0.0, op0=MULT, op1=ADD
+            )
+
         def h_last_prod(t, g, a=0, b=None):
             lo, w = HG[g]
             if b is None:
@@ -206,6 +214,17 @@ def tile_lowrankconv3d_kernel(tc, x, U_kh, U_kw, U_kd, U_c_in, U_c_out, bias, ou
             need_zr(g)
             s = lo + SLICE
             nc.scalar.activation(out=zr[g][1][:, t, a:b], in_=v[t][:, s + a : s + b], func=COPY, scale=tap(t, KH + 2))
+
+        def v_join(g, a, b):
+            w = HG[g][1]
+            if g not in y3g:
+                y3g[g] = ypool.tile([P, w, PACK], BF16, name="y3g_%d" % g, tag="y3g", align_bytes=64)
+            nc.vector.tensor_tensor(
+                out=y3g[g][:, a:b, :].rearrange("p (c i) t -> p c t i", i=4),
+                in0=zr[g][0][:, :, a:b].rearrange("p t (c i) -> p c t i", i=4),
+                in1=zr[g][1][:, :, a:b].rearrange("p t (c i) -> p c t i", i=4),
+                op=ADD,
+            )
 
         def h_join(g, a, b):
             w = HG[g][1]
@@ -405,12 +424,12 @@ def tile_lowrankconv3d_kernel(tc, x, U_kh, U_kw, U_kd, U_c_in, U_c_out, bias, ou
         h_last_prod(0, 0)
         h_last_prod(1, 0)
         for t in (2, 3):
-            h_centre(t, 0)
+            h_centre_g(t, 0)
             h_last_prod(t, 0)
+        x_regroup(4, "G", 0, 256)
         h_join(0, 0, 256)
         d_centre(2, 512)
         d_centre(3, 512)
-        x_regroup(4, "G", 0, 256)
         x_regroup(3, "S", 256, 512)
 
         d_pair(0, 1, 512)
@@ -449,7 +468,7 @@ def tile_lowrankconv3d_kernel(tc, x, U_kh, U_kw, U_kd, U_c_in, U_c_out, bias, ou
             h_last_prod(t, 1, 256, 512)
         for t in (0, 1):
             z_copy(t, 1, 256, 512)
-        h_join(1, 256, 512)
+        h_join(1, 256, 384)
         for o in range(NT):
             mm2(o, 0)
 
@@ -457,10 +476,11 @@ def tile_lowrankconv3d_kernel(tc, x, U_kh, U_kw, U_kd, U_c_in, U_c_out, bias, ou
         x_regroup(4, "S", 256, 512)
         w_centre(0, 2)
         w_centre(1, 2)
-        outp(0, 0, "S")
         d_pair(2, 3, 1024)
         w_centre(2, 2)
         w_centre(3, 2)
+        v_join(1, 384, 512)
+        outp(0, 0, "S")
         outp(1, 0, "S")
         outp(2, 0, "S")
         outp(3, 0, "S")
@@ -494,11 +514,8 @@ def tile_lowrankconv3d_kernel(tc, x, U_kh, U_kw, U_kd, U_c_in, U_c_out, bias, ou
             h_last_prod(t, 2, 256, 512)
         for t in (0, 1):
             z_copy(t, 2, 256, 512)
-        h_join(2, 256, 512)
+        h_join(2, 256, 384)
         mm2(3, 1)
-        outp(0, 1, "S")
-        outp(1, 1, "S")
-
         d_pair(0, 1, 1536)
         w_centre(0, 3)
         w_centre(1, 3)
@@ -507,6 +524,9 @@ def tile_lowrankconv3d_kernel(tc, x, U_kh, U_kw, U_kd, U_c_in, U_c_out, bias, ou
         d_pair(2, 3, 1536)
         w_centre(2, 3)
         w_centre(3, 3)
+        v_join(2, 384, 512)
+        outp(0, 1, "S")
+        outp(1, 1, "S")
         outp(2, 1, "S")
         outp(3, 1, "S")
         w_pair(0, 1, 3)
@@ -515,6 +535,7 @@ def tile_lowrankconv3d_kernel(tc, x, U_kh, U_kw, U_kd, U_c_in, U_c_out, bias, ou
             mm2(o, 2)
         h_pe(TPE, 3, (0, 1), start=True, stop=True)
         h_pe(TPE, 4, (2,), stop=True)
+        h_pe(TPE, 5, (1, 2), stop=True)
         h_centre(1, 3)
         h_centre(1, 4)
         outp(0, 2, "S")
@@ -538,7 +559,6 @@ def tile_lowrankconv3d_kernel(tc, x, U_kh, U_kw, U_kd, U_c_in, U_c_out, bias, ou
         y_quant(3)
         for o in range(NT):
             mm2(o, 3)
-        h_pe(TPE, 5, (1, 2), stop=True)
         h_centre(2, 5)
         h_centre(3, 5)
         ycopy(4)

from contextlib import ExitStack

import concourse.mybir as mybir
from concourse.masks import make_identity

F32 = mybir.dt.float32
BF16 = mybir.dt.bfloat16
U32 = mybir.dt.uint32
U8 = mybir.dt.uint8
FP8X4 = mybir.dt.float8_e4m3fn_x4
MULT = mybir.AluOpType.mult
ADD = mybir.AluOpType.add
COPY = mybir.ActivationFunctionType.Copy
IDENT = mybir.ActivationFunctionType.Identity

P = 128
PACK = 4
NPOS = 2048
SLICE = 256
ROW = 16
CHUNK = 512
NT = 4
KH = 0
KW = 3
KB = 6
NSMALL = 7
KD = 7
TPE = 0
TV = (1, 2, 3)

FLOPS = 2 * 2 * 512 * 512 * NPOS + 2 * 9 * 512 * NPOS

XP = ((0, 256), (256, 256), (512, 512), (1024, 512), (1536, 512))
GJOIN = (0, 1, 2)
HG = ((0, 256), (256, 512), (768, 512), (1792, 256), (1280, 256), (1536, 256))


def tile_lowrankconv3d_kernel(tc, x, U_kh, U_kw, U_kd, U_c_in, U_c_out, bias, out):
    nc = tc.nc
    xv = x.rearrange("b c h w d -> (b c) (h w d)").rearrange("(p j) n -> p j n", j=PACK)
    uinv = U_c_in.rearrange("(p j) r -> p j r", j=PACK)
    uoutv = U_c_out.rearrange("(j p) o -> p j o", p=P)
    outv = out.rearrange("b o h w d -> (b o) (h w d)")

    with ExitStack() as ctx:
        keep = ctx.enter_context(tc.tile_pool(name="keep", bufs=1))
        xgp = ctx.enter_context(tc.tile_pool(name="xgp", bufs=1))
        upool = ctx.enter_context(tc.tile_pool(name="upool", bufs=8))
        zpool = ctx.enter_context(tc.tile_pool(name="zpool", bufs=10))
        zrpool = ctx.enter_context(tc.tile_pool(name="zrpool", bufs=1))
        ypool = ctx.enter_context(tc.tile_pool(name="ypool", bufs=3))
        opool = ctx.enter_context(tc.tile_pool(name="opool", bufs=12))
        ps = ctx.enter_context(tc.psum_pool(name="ps", bufs=8))
        ctx.enter_context(tc.manual_schedule())

        smalld = keep.tile([P, 512], BF16, name="smalld")
        small = keep.tile([P, 512], BF16, name="small")
        warm = keep.tile([P, 8], F32, name="warm")
        warm2 = keep.tile([P, 8], F32, name="warm2")
        ident = keep.tile([P, P], BF16, name="ident")
        ident32 = keep.tile([P, P], F32, name="ident32")
        diag = {}
        tapsd = keep.tile([P, NT, 3], F32, name="tapsd")
        taps = keep.tile([P, NT, NSMALL], F32, name="taps")
        uin_raw = keep.tile([P, PACK, 512], BF16, name="uin_raw")
        uin_g = keep.tile([P, 512, PACK], BF16, name="uin_g", align_bytes=64)
        uin_c = keep.tile([P, 512], U32, name="uin_c", align_bytes=64)
        uin_s = keep.tile([P, 512], U8, name="uin_s", align_bytes=64)
        uout_raw = keep.tile([P, PACK, 512], BF16, name="uout_raw")
        uout_g = keep.tile([P, 512, PACK], BF16, name="uout_g", align_bytes=64)
        uout_c = keep.tile([P, 512], U32, name="uout_c", align_bytes=64)
        uout_s = keep.tile([P, 512], U8, name="uout_s", align_bytes=64)
        xraw = [keep.tile([P, PACK, XP[i][1]], BF16, name="xraw%d" % i) for i in range(len(XP))]
        xc = [keep.tile([P, XP[i][1]], U32, name="xc%d" % i, align_bytes=64) for i in range(len(XP))]
        xs = [keep.tile([P, XP[i][1]], U8, name="xs%d" % i, align_bytes=64) for i in range(len(XP))]
        v = [keep.tile([P, NPOS], F32, name="v%d" % t) for t in range(NT)]
        xg = {}
        y0 = {}
        u = {}
        z = {}
        y3 = {}
        y3g = {}
        yc = {}
        ys = {}
        po = {}
        ph = {}
        pr = {}
        zr = {}

        def tap(t, k):
            if k >= KD:
                return tapsd[:, t, k - KD : k - KD + 1]
            return taps[:, t, k : k + 1]

        def regroup(eng, dst, src):
            if eng == "G":
                nc.gpsimd.tensor_scalar(
                    out=dst, in0=src.rearrange("p t w -> p w t"), scalar1=1.0, scalar2=0.0, op0=MULT, op1=ADD
                )
                return
            d4 = dst.rearrange("p (c i) t -> p c t i", i=4)
            s4 = src.rearrange("p t (c i) -> p c t i", i=4)
            if eng == "V":
                nc.vector.tensor_copy(out=d4, in_=s4)
            else:
                nc.scalar.copy(out=d4, in_=s4)

        def quantise(codes, scales, grouped):
            nc.vector.quantize_mx(
                out=codes.bitcast(FP8X4), scales=scales, in_=grouped.rearrange("p w t -> p (w t)")
            )

        def x_regroup(i, eng, a=0, b=None):
            w = XP[i][1]
            if b is None:
                b = w
            if i not in xg:
                xg[i] = xgp.tile([P, w, PACK], BF16, name="xg%d" % i, tag="xgodd" if i == 3 else "xg", align_bytes=64)
            regroup(eng, xg[i][:, a:b, :], xraw[i][:, :, a:b])

        def x_quant(i):
            quantise(xc[i][:], xs[i][:], xg[i][:])

        def mm1(t, *pieces):
            lo = XP[pieces[0]][0]
            w = sum(XP[i][1] for i in pieces)
            y0[(t, lo)] = ps.tile([P, w], F32, name="y0_%d_%d" % (t, lo), tag="ps")
            for i in pieces:
                o = XP[i][0] - lo
                nc.tensor.matmul_mx(
                    out=y0[(t, lo)][:, o : o + XP[i][1]],
                    lhsT=uin_c[:, t * P : (t + 1) * P].bitcast(FP8X4),
                    lhsT_scale=uin_s[:, t * P : (t + 1) * P],
                    rhs=xc[i][:].bitcast(FP8X4),
                    rhs_scale=xs[i][:],
                    start=True,
                    stop=True,
                )

        def u_part(t, lo):
            c = lo // CHUNK
            if (t, c) not in u:
                u[(t, c)] = upool.tile([P, CHUNK], F32, name="u_%d_%d" % (t, c), tag="u")
            o = lo % CHUNK
            return u[(t, c)][:, o : o + y0[(t, lo)].shape[1]]

        def d_centre(t, lo):
            nc.scalar.activation(out=u_part(t, lo), in_=y0[(t, lo)][:], func=COPY, scale=tap(t, KD + 1))

        def d_side(t, lo, k):
            uu = u_part(t, lo).rearrange("p (r d) -> p r d", d=ROW)
            yy = y0[(t, lo)][:].rearrange("p (r d) -> p r d", d=ROW)
            if k == 0:
                dst, src = uu[:, :, 1:ROW], yy[:, :, 0 : ROW - 1]
            else:
                dst, src = uu[:, :, 0 : ROW - 1], yy[:, :, 1:ROW]
            nc.vector.scalar_tensor_tensor(out=dst, in0=src, scalar=tap(t, KD + k), in1=dst, op0=MULT, op1=ADD)

        def d_pair(a, b, i):
            d_side(a, i, 0)
            d_side(b, i, 0)
            d_side(a, i, 2)
            d_side(b, i, 2)

        def w_centre(t, c):
            nc.scalar.activation(
                out=v[t][:, c * CHUNK : (c + 1) * CHUNK], in_=u[(t, c)][:], func=COPY, scale=tap(t, KW + 1)
            )

        def w_side(t, c, k):
            vv = v[t][:, c * CHUNK : (c + 1) * CHUNK].rearrange("p (s n) -> p s n", n=SLICE)
            uu = u[(t, c)][:].rearrange("p (s n) -> p s n", n=SLICE)
            if k == 0:
                dst, src = vv[:, :, ROW:SLICE], uu[:, :, 0 : SLICE - ROW]
            else:
                dst, src = vv[:, :, 0 : SLICE - ROW], uu[:, :, ROW:SLICE]
            nc.vector.scalar_tensor_tensor(out=dst, in0=src, scalar=tap(t, KW + k), in1=dst, op0=MULT, op1=ADD)

        def w_pair(a, b, c):
            w_side(a, c, 0)
            w_side(b, c, 0)
            w_side(a, c, 2)
            w_side(b, c, 2)

        def need_zr(g):
            if g not in zr:
                w = HG[g][1]
                zr[g] = (
                    zrpool.tile([P, NT, w], F32, name="zz_%d" % g, tag="zz"),
                    zrpool.tile([P, NT, w], F32, name="rr_%d" % g, tag="rr"),
                )

        def h_centre(t, g):
            lo, w = HG[g]
            if g in GJOIN:
                need_zr(g)
                z[(t, g)] = zr[g][0][:, t, :]
            else:
                z[(t, g)] = zpool.tile([P, w], F32, name="z_%d_%d" % (t, g), tag="z")
            nc.scalar.activation(out=z[(t, g)][:, 0:w], in_=v[t][:, lo : lo + w], func=COPY, scale=tap(t, KH + 1))

        def h_centre_g(t, g):
            lo, w = HG[g]
            need_zr(g)
            z[(t, g)] = zr[g][0][:, t, :]
            nc.gpsimd.tensor_scalar(
                out=z[(t, g)], in0=v[t][:, lo : lo + w], scalar1=tap(t, KH + 1), scalar2=0.0, op0=MULT, op1=ADD
            )

        def h_last_prod(t, g, a=0, b=None):
            lo, w = HG[g]
            if b is None:
                b = w
            need_zr(g)
            s = lo + SLICE
            nc.scalar.activation(out=zr[g][1][:, t, a:b], in_=v[t][:, s + a : s + b], func=COPY, scale=tap(t, KH + 2))

        def v_join(g, a, b):
            w = HG[g][1]
            if g not in y3g:
                y3g[g] = ypool.tile([P, w, PACK], BF16, name="y3g_%d" % g, tag="y3g", align_bytes=64)
            nc.vector.tensor_tensor(
                out=y3g[g][:, a:b, :].rearrange("p (c i) t -> p c t i", i=4),
                in0=zr[g][0][:, :, a:b].rearrange("p t (c i) -> p c t i", i=4),
                in1=zr[g][1][:, :, a:b].rearrange("p t (c i) -> p c t i", i=4),
                op=ADD,
            )

        def h_join(g, a, b):
            w = HG[g][1]
            if g not in y3g:
                y3g[g] = ypool.tile([P, w, PACK], BF16, name="y3g_%d" % g, tag="y3g", align_bytes=64)
            nc.gpsimd.tensor_tensor(
                out=y3g[g][:, a:b, :].rearrange("p (c i) t -> p c t i", i=4),
                in0=zr[g][0][:, :, a:b].rearrange("p t (c i) -> p c t i", i=4),
                in1=zr[g][1][:, :, a:b].rearrange("p t (c i) -> p c t i", i=4),
                op=ADD,
            )

        def need_y3(g):
            if g not in y3:
                y3[g] = ypool.tile([P, NT, HG[g][1]], BF16, name="y3_%d" % g, tag="y3")

        def h_pe(t, g, ks, start=False, stop=False):
            lo, w = HG[g]
            if start:
                ph[(t, g)] = ps.tile([P, w], F32, name="ph_%d_%d" % (t, g), tag="ps")
            for n, k in enumerate(ks):
                s = lo + (k - 1) * SLICE
                nc.tensor.matmul(
                    out=ph[(t, g)][:], lhsT=diag[(t, k)][:], rhs=v[t][:, s : s + w],
                    start=start and n == 0, stop=stop and n == len(ks) - 1,
                )

        def h_pe_part(t, g, a, b):
            lo = HG[g][0]
            ph[(t, g, a)] = ps.tile([P, b - a], F32, name="ph_%d_%d_%d" % (t, g, a), tag="ps")
            for k in (1, 0):
                s = lo + (k - 1) * SLICE
                nc.tensor.matmul(
                    out=ph[(t, g, a)][:], lhsT=diag[(t, k)][:], rhs=v[t][:, s + a : s + b], start=k == 1, stop=k == 0
                )

        def z_copy(t, g, a, b):
            need_zr(g)
            nc.scalar.copy(out=zr[g][0][:, t, a:b], in_=ph[(t, g, a)][:])

        def make_diag(t, k):
            diag[(t, k)] = keep.tile([P, P], F32, name="diag%d_%d" % (t, k))
            nc.scalar.activation(out=diag[(t, k)][:], in_=ident32[:], func=COPY, scale=tap(t, KH + k))

        def h_last(t, g):
            lo, w = HG[g]
            need_y3(g)
            nc.vector.scalar_tensor_tensor(
                out=y3[g][:, t, :], in0=v[t][:, lo + SLICE : lo + w + SLICE], scalar=tap(t, KH + 2), in1=ph[(t, g)][:],
                op0=MULT, op1=ADD,
            )

        def ycopy(g):
            need_y3(g)
            nc.scalar.copy(out=y3[g][:, TPE, :], in_=ph[(TPE, g)][:])

        def h_side(t, g, k):
            lo, w = HG[g]
            need_y3(g)
            zz = z[(t, g)][:, 0:w]
            last = lo + w == NPOS
            if k == 0:
                a = max(lo, SLICE)
                dst = y3[g][:, t, :] if last else zz[:, a - lo : w]
                nc.vector.scalar_tensor_tensor(
                    out=dst, in0=v[t][:, a - SLICE : lo + w - SLICE], scalar=tap(t, KH), in1=zz[:, a - lo : w],
                    op0=MULT, op1=ADD,
                )
            else:
                nc.vector.scalar_tensor_tensor(
                    out=y3[g][:, t, :], in0=v[t][:, lo + SLICE : lo + w + SLICE], scalar=tap(t, KH + 2), in1=zz[:],
                    op0=MULT, op1=ADD,
                )

        def h_prod(t, g, k):
            lo, w = HG[g]
            s = lo - SLICE if k == 0 else lo + SLICE
            pr[(t, g, k)] = zpool.tile([P, w], F32, name="p%d_%d_%d" % (k, t, g), tag="p")
            nc.scalar.activation(out=pr[(t, g, k)][:], in_=v[t][:, s : s + w], func=COPY, scale=tap(t, KH + k))

        def h_add(t, g, k):
            need_y3(g)
            zz = z[(t, g)]
            dst = y3[g][:, t, :] if k == 2 else zz[:]
            nc.gpsimd.tensor_tensor(out=dst, in0=zz[:], in1=pr[(t, g, k)][:], op=ADD)

        def h_triple(g):
            for k in (0, 2):
                for t in TV:
                    h_side(t, g, k)

        def y_regroup(g, eng, a=0, b=None):
            w = HG[g][1]
            if b is None:
                b = w
            if g not in y3g:
                y3g[g] = ypool.tile([P, w, PACK], BF16, name="y3g_%d" % g, tag="y3g", align_bytes=64)
            regroup(eng, y3g[g][:, a:b, :], y3[g][:, :, a:b])

        def y_quant(g):
            w = HG[g][1]
            yc[g] = ypool.tile([P, w], U32, name="yc_%d" % g, tag="yc", align_bytes=64)
            ys[g] = ypool.tile([P, w], U8, name="ys_%d" % g, tag="ys", align_bytes=64)
            quantise(yc[g][:], ys[g][:], y3g[g][:])

        def mm2(o, g):
            w = HG[g][1]
            po[(o, g)] = ps.tile([P, w], F32, name="po_%d_%d" % (o, g), tag="ps")
            nc.tensor.matmul_mx(
                out=po[(o, g)][:],
                lhsT=uout_c[:, o * P : (o + 1) * P].bitcast(FP8X4),
                lhsT_scale=uout_s[:, o * P : (o + 1) * P],
                rhs=yc[g][:].bitcast(FP8X4),
                rhs_scale=ys[g][:],
                start=True,
                stop=True,
            )

        def outp(o, g, eng):
            lo, w = HG[g]
            ost = opool.tile([P, w], F32, name="ost_%d_%d" % (o, g), tag="ost")
            if eng == "V":
                nc.vector.tensor_scalar(out=ost[:], in0=po[(o, g)][:], scalar1=tap(o, KB), scalar2=None, op0=ADD)
            else:
                nc.scalar.activation(out=ost[:], in_=po[(o, g)][:], func=IDENT, bias=tap(o, KB), scale=1.0)
            nc.sync.dma_start(out=outv[o * P : (o + 1) * P, lo : lo + w], in_=ost[:])

        nc.gpsimd.memset(smalld[:].bitcast(F32), 0.0)
        nc.gpsimd.memset(small[:].bitcast(F32), 0.0)
        nc.vector.memset(warm[:], 0.0)
        nc.scalar.activation(out=warm2[:], in_=warm[:], func=COPY, scale=1.0)
        make_identity(nc, ident[:])
        make_identity(nc, ident32[:])
        nc.sync.dma_start(out=xraw[0][:], in_=xv[:, :, XP[0][0] : XP[0][0] + XP[0][1]])
        nc.sync.dma_start(out=uin_raw[:, :, 0:256], in_=uinv[:, :, 0:256])
        nc.sync.dma_start(out=smalld[0:3, :], in_=U_kd)
        nc.sync.dma_start(out=uin_raw[:, :, 256:512], in_=uinv[:, :, 256:512])
        nc.sync.dma_start(out=xraw[1][:], in_=xv[:, :, XP[1][0] : XP[1][0] + XP[1][1]])
        nc.sync.dma_start(out=small[KW : KW + 3, :], in_=U_kw)
        nc.sync.dma_start(out=small[KH : KH + 3, :], in_=U_kh)
        nc.sync.dma_start(out=small[KB : KB + 1, :], in_=bias.rearrange("(a n) -> a n", a=1))
        nc.sync.dma_start(out=xraw[2][:], in_=xv[:, :, XP[2][0] : XP[2][0] + XP[2][1]])
        for i in range(3, len(XP)):
            nc.sync.dma_start(out=xraw[i][:], in_=xv[:, :, XP[i][0] : XP[i][0] + XP[i][1]])
        nc.sync.dma_start(out=uout_raw[:], in_=uoutv)

        def spread(dst, src, n, name):
            tp = ps.tile([P, NT, P], BF16, name=name, tag="ps")
            for t in range(NT):
                nc.tensor.transpose(tp[:, t, :], src[:, t * P : (t + 1) * P], ident[:])
            nc.scalar.copy(out=dst[:], in_=tp[:, :, 0:n])

        x_regroup(0, "V")
        x_quant(0)
        regroup("V", uin_g[:, 0:256, :], uin_raw[:, :, 0:256])
        spread(tapsd, smalld, 3, "tpd")
        regroup("S", uin_g[:, 256:512, :], uin_raw[:, :, 256:512])
        quantise(uin_c[:, 0:256], uin_s[:, 0:256], uin_g[:, 0:256, :])
        x_regroup(1, "V")
        for t in (0, 1):
            mm1(t, 0)
        for t in (0, 1):
            d_centre(t, 0)
        quantise(uin_c[:, 256:512], uin_s[:, 256:512], uin_g[:, 256:512, :])
        x_quant(1)
        for t in (0, 1):
            mm1(t, 1)
        for t in (0, 1):
            d_centre(t, 256)
        for t in (2, 3):
            mm1(t, 0, 1)
        for t in (2, 3):
            d_centre(t, 0)
        spread(taps, small, NSMALL, "tp")
        x_regroup(2, "G")
        x_regroup(3, "G", 0, 256)

        d_pair(0, 1, 0)
        d_pair(0, 1, 256)
        w_centre(0, 0)
        w_centre(1, 0)
        d_pair(2, 3, 0)
        w_centre(2, 0)
        w_centre(3, 0)
        regroup("S", uout_g[:, 0:256, :], uout_raw[:, :, 0:256])
        for t, k in ((0, 1), (0, 0), (1, 1), (1, 0), (0, 2)):
            make_diag(t, k)
        x_quant(2)
        for t in range(NT):
            mm1(t, 2)
        w_pair(0, 1, 0)
        h_centre(0, 0)
        h_centre(1, 0)
        w_pair(2, 3, 0)
        d_centre(0, 512)
        d_centre(1, 512)
        h_last_prod(0, 0)
        h_last_prod(1, 0)
        for t in (2, 3):
            h_centre_g(t, 0)
            h_last_prod(t, 0)
        x_regroup(4, "G", 0, 256)
        h_join(0, 0, 256)
        d_centre(2, 512)
        d_centre(3, 512)
        x_regroup(3, "S", 256, 512)

        d_pair(0, 1, 512)
        w_centre(0, 1)
        w_centre(1, 1)
        d_pair(2, 3, 512)
        w_centre(2, 1)
        w_centre(3, 1)
        regroup("S", uout_g[:, 256:512, :], uout_raw[:, :, 256:512])
        x_quant(3)
        for t in range(NT):
            mm1(t, 3)
        w_pair(0, 1, 1)
        for a in (0, 256):
            for t in (0, 1):
                h_pe_part(t, 1, a, a + 256)
        d_centre(0, 1024)
        d_centre(1, 1024)
        h_last_prod(0, 1)
        h_last_prod(1, 1)
        w_pair(2, 3, 1)
        y_quant(0)
        h_centre(2, 1)
        h_centre(3, 1)
        quantise(uout_c[:], uout_s[:], uout_g[:])
        h_side(2, 1, 0)
        h_side(3, 1, 0)
        for t in (2, 3):
            h_last_prod(t, 1, 0, 256)
        for t in (0, 1):
            z_copy(t, 1, 0, 256)
        h_join(1, 0, 256)
        d_centre(2, 1024)
        d_centre(3, 1024)
        for t in (2, 3):
            h_last_prod(t, 1, 256, 512)
        for t in (0, 1):
            z_copy(t, 1, 256, 512)
        h_join(1, 256, 384)
        for o in range(NT):
            mm2(o, 0)

        d_pair(0, 1, 1024)
        x_regroup(4, "S", 256, 512)
        w_centre(0, 2)
        w_centre(1, 2)
        d_pair(2, 3, 1024)
        w_centre(2, 2)
        w_centre(3, 2)
        v_join(1, 384, 512)
        outp(0, 0, "S")
        outp(1, 0, "S")
        outp(2, 0, "S")
        outp(3, 0, "S")
        x_quant(4)
        for t in range(NT):
            mm1(t, 4)
        w_pair(0, 1, 2)
        for a in (0, 256):
            for t in (0, 1):
                h_pe_part(t, 2, a, a + 256)
        d_centre(0, 1536)
        d_centre(1, 1536)
        h_last_prod(0, 2)
        h_last_prod(1, 2)
        w_pair(2, 3, 2)
        y_quant(1)
        for o in range(3):
            mm2(o, 1)
        h_centre(2, 2)
        h_centre(3, 2)
        h_side(2, 2, 0)
        h_side(3, 2, 0)
        for t in (2, 3):
            h_last_prod(t, 2, 0, 256)
        for t in (0, 1):
            z_copy(t, 2, 0, 256)
        h_join(2, 0, 256)
        d_centre(2, 1536)
        d_centre(3, 1536)
        for t in (2, 3):
            h_last_prod(t, 2, 256, 512)
        for t in (0, 1):
            z_copy(t, 2, 256, 512)
        h_join(2, 256, 384)
        mm2(3, 1)
        d_pair(0, 1, 1536)
        w_centre(0, 3)
        w_centre(1, 3)
        h_pe(TPE, 4, (1, 0), start=True)
        h_pe(TPE, 5, (0,), start=True)
        d_pair(2, 3, 1536)
        w_centre(2, 3)
        w_centre(3, 3)
        v_join(2, 384, 512)
        outp(0, 1, "S")
        outp(1, 1, "S")
        outp(2, 1, "S")
        outp(3, 1, "S")
        w_pair(0, 1, 3)
        y_quant(2)
        for o in range(NT):
            mm2(o, 2)
        h_pe(TPE, 3, (0, 1), start=True, stop=True)
        h_pe(TPE, 4, (2,), stop=True)
        h_pe(TPE, 5, (1, 2), stop=True)
        h_centre(1, 3)
        h_centre(1, 4)
        outp(0, 2, "S")
        h_centre(1, 5)
        w_pair(2, 3, 3)
        outp(1, 2, "S")
        h_centre(2, 3)
        h_centre(3, 3)
        outp(2, 2, "S")
        h_centre(2, 4)
        h_centre(3, 4)
        ycopy(3)
        outp(3, 2, "S")
        for g in (3, 4, 5):
            h_side(1, g, 0)
        for g in (3, 4):
            h_side(2, g, 0)
            h_side(3, g, 0)
        y_regroup(3, "V")
        h_side(1, 4, 2)
        y_quant(3)
        for o in range(NT):
            mm2(o, 3)
        h_centre(2, 5)
        h_centre(3, 5)
        ycopy(4)
        h_side(2, 4, 2)
        h_side(3, 4, 2)
        outp(0, 3, "S")
        outp(1, 3, "S")
        y_regroup(4, "S")
        h_side(2, 5, 0)
        h_side(3, 5, 0)
        for t in TV:
            h_side(t, 5, 2)
        ycopy(5)
        outp(2, 3, "S")
        outp(3, 3, "S")
        y_quant(4)
        for o in range(NT):
            mm2(o, 4)
        y_regroup(5, "V")
        outp(0, 4, "S")
        outp(1, 4, "S")
        y_quant(5)
        for o in range(NT):
            mm2(o, 5)
        outp(2, 4, "V")
        outp(3, 4, "S")
        outp(0, 5, "V")
        outp(1, 5, "S")
        outp(2, 5, "V")
        outp(3, 5, "S")
